import numpy as np
import ml_dtypes


def mxq(x, axis, fmt="e4m3"):
    dtype, down = {"e4m3": (ml_dtypes.float8_e4m3fn, 7), "e5m2": (ml_dtypes.float8_e5m2, 14)}[fmt]
    v = np.moveaxis(np.asarray(x, np.float32).astype(ml_dtypes.bfloat16).astype(np.float64), axis, -1)
    blocks = v.reshape(v.shape[:-1] + (-1, 32))
    amax = np.abs(blocks).max(-1, keepdims=True)
    byte = np.maximum(np.where(amax > 0, np.frexp(amax)[1] - 1 + 127, 0) - down, 1)
    scale = np.exp2(byte - 127.0)
    codes = (blocks / scale).astype(np.float32).astype(dtype).astype(np.float64)
    return np.moveaxis((codes * scale).reshape(v.shape), -1, axis)


WIDE = False


def mx_kscale(k):
    if not WIDE:
        return np.ones(k)
    levels = np.array([10, -10, 5, -5, 0])
    a = np.random.permutation(np.resize(levels, k // 512 * 4)).reshape(k // 512, 4)
    idx = np.arange(k)
    return np.exp2(a[idx // 512, idx % 128 // 32])


BF16 = ml_dtypes.bfloat16


def bf(x):
    return np.asarray(x, np.float32).astype(BF16)


def f64(x):
    return np.asarray(x).astype(np.float64)


B, S, D_IN, D_OUT = 4, 256, 2048, 2048
THRESHOLD = 2.0 / 3.0


def _quantize_1_58_bit(weight):
    scale = np.clip(np.mean(np.abs(weight)), 1e-5, 1000.0)
    weight_norm = np.clip(weight / scale, -10.0, 10.0)
    q = np.where(weight_norm > THRESHOLD, 1.0, np.where(weight_norm < -THRESHOLD, -1.0, 0.0))
    return q, scale


def setup_inputs():
    s = mx_kscale(D_IN)
    r = 1.0 / s**2
    keep = r >= 0.5 * np.mean(r)
    g = np.exp2(np.round(-np.log2(np.mean(r) * np.sqrt(np.mean(keep * s**2)))))
    return {"x": bf(np.random.standard_normal((B, S, D_IN)) * s),
            "weight": bf(np.random.standard_normal((D_OUT, D_IN)) * 1.5 / np.sqrt(D_IN) * r * g),
            "bias": bf(np.random.standard_normal(D_OUT) * 0.1)}


def reference(x, weight, bias):
    q, scale = _quantize_1_58_bit(f64(weight))
    weight_q = q * scale
    out = (mxq(f64(x), 2, "e4m3") @ mxq(weight_q, 1, "e4m3").T) + f64(bias)
    return out

@@ -1,0 +1,169 @@
+from contextlib import ExitStack
+
+import concourse.bass as bass
+import concourse.mybir as mybir
+import concourse.tile as tile
+from concourse.masks import make_identity
+
+F32 = mybir.dt.float32
+BF16 = mybir.dt.bfloat16
+I32 = mybir.dt.int32
+U32 = mybir.dt.uint32
+U8 = mybir.dt.uint8
+FP8X4 = mybir.dt.float8_e4m3fn_x4
+ALU = mybir.AluOpType
+ACT = mybir.ActivationFunctionType
+AX = mybir.AxisListType
+
+P = 128
+M_ROWS = 1024
+D_IN = 2048
+D_OUT = 2048
+N_W = D_OUT * D_IN
+FLOPS = 2 * M_ROWS * D_IN * D_OUT
+
+N_OT = D_OUT // P
+N_MT = M_ROWS // P
+N_C = D_IN // 512
+N_J = D_OUT // 512
+S_ABS_TILES = (0, 1, 2, 3)
+
+
+def tile_bitnetlinear_kernel(tc, x, weight, bias, out):
+    nc = tc.nc
+    xf = x.flatten_outer_dims()
+    of = out.flatten_outer_dims()
+    with ExitStack() as ctx:
+        const = ctx.enter_context(tc.tile_pool(name="const", bufs=1))
+        keep = ctx.enter_context(tc.tile_pool(name="keep", bufs=1))
+        nat = ctx.enter_context(tc.tile_pool(name="nat", bufs=5))
+        xgp = ctx.enter_context(tc.tile_pool(name="xgp", bufs=2))
+        osp = ctx.enter_context(tc.tile_pool(name="osp", bufs=4))
+        psum = ctx.enter_context(tc.psum_pool(name="psum", bufs=1))
+
+        ident = const.tile([P, P], F32, name="ident")
+        make_identity(nc, ident[:])
+        ones_bf = const.tile([P, P], BF16, name="ones_bf")
+        nc.vector.memset(ones_bf[:], 1.0)
+        ones_f = const.tile([P, P], F32, name="ones_f")
+        nc.vector.memset(ones_f[:], 1.0)
+        part_s = const.tile([P, 4], F32, name="part_s")
+        junk = const.tile([P, 1], F32, name="junk")
+        nc.vector.memset(junk[:], 0.0)
+        junk2 = const.tile([P, 1], F32, name="junk2")
+        nc.scalar.activation(out=junk2[:], in_=junk[:], func=ACT.Abs)
+        bias_bc = const.tile([P, D_OUT], BF16, name="bias_bc")
+
+        g_t = [keep.tile([P, 8192], BF16, name="g%d" % j, align_bytes=64) for j in range(N_J)]
+        a_t = [keep.tile([P, 8192], BF16, name="a%d" % j, align_bytes=64) for j in range(N_J)]
+        w_codes = keep.tile([P, N_C * D_OUT], U32, name="w_codes", align_bytes=64)
+        w_scales = keep.tile([P, N_C * D_OUT], U8, name="w_scales", align_bytes=64)
+        x_codes = keep.tile([P, N_MT * 512], U32, name="x_codes", align_bytes=64)
+        x_scales = keep.tile([P, N_MT * 512], U8, name="x_scales", align_bytes=64)
+
+        sum_ps = psum.tile([P, 512], F32, tag="b6", name="sum_ps")
+        tot_ps = psum.tile([P, 512], F32, tag="b7", name="tot_ps")
+
+        state = {"bank": 0}
+
+        def transpose_tile(src, dst_words, col0, ncols_total, evac_v):
+            sv = src[:].bitcast(F32)
+            for b in range(2):
+                bank = state["bank"] % 6
+                idx = state["bank"]
+                state["bank"] = idx + 1
+                tb = psum.tile([P, 512], F32, tag="b%d" % bank, name="tp%d" % idx)
+                for q in range(4):
+                    c = 2 * b + q // 2
+                    u = q % 2
+                    nc.tensor.transpose(
+                        tb[:, 128 * q : 128 * (q + 1)],
+                        sv[:, 256 * c + 128 * u : 256 * c + 128 * u + 128],
+                        ident[:],
+                    )
+                src_ap = tb[:].rearrange("p (c u o) -> p c o u", c=2, u=2)
+                dst_ap = dst_words[:, 2 * b : 2 * b + 2, col0 : col0 + 128, :]
+                if evac_v and idx % 3 == 2:
+                    nc.vector.tensor_copy(out=dst_ap, in_=src_ap)
+                else:
+                    nc.scalar.copy(out=dst_ap, in_=src_ap)
+
+        pe_tiles = [i for i in range(N_OT) if i not in S_ABS_TILES]
+        for i in range(N_OT):
+            j = i // 4
+            r = i % 4
+            wn = nat.tile([P, D_IN], BF16, tag="nat", name="wn%d" % i)
+            nc.sync.dma_start(out=wn[:], in_=weight[P * i : P * (i + 1), :])
+            gw = g_t[j][:].bitcast(F32).rearrange("p (c o u) -> p c o u", c=4, u=2)
+            transpose_tile(wn, gw, 128 * r, 512, True)
+            g_bf = g_t[j][:].rearrange("p (c e) -> p c e", c=4)[:, :, 512 * r : 512 * (r + 1)]
+            a_bf = a_t[j][:].rearrange("p (c e) -> p c e", c=4)[:, :, 512 * r : 512 * (r + 1)]
+            if i in S_ABS_TILES:
+                k = S_ABS_TILES.index(i)
+                nc.scalar.activation(out=a_bf, in_=g_bf, func=ACT.Abs, accum_out=part_s[:, k : k + 1])
+            else:
+                g_i = g_t[j][:].bitcast(I32).rearrange("p (c e) -> p c e", c=4)[:, :, 256 * r : 256 * (r + 1)]
+                a_i = a_t[j][:].bitcast(I32).rearrange("p (c e) -> p c e", c=4)[:, :, 256 * r : 256 * (r + 1)]
+                nc.vector.tensor_scalar(out=a_i, in0=g_i, scalar1=0x7FFF7FFF, scalar2=None, op0=ALU.bitwise_and)
+                for c in range(N_C):
+                    nc.tensor.matmul(
+                        sum_ps[:],
+                        lhsT=ones_bf[:],
+                        rhs=a_t[j][:, 2048 * c + 512 * r : 2048 * c + 512 * (r + 1)],
+                        start=(i == pe_tiles[0] and c == 0),
+                        stop=(i == pe_tiles[-1] and c == N_C - 1),
+                    )
+            nc.vector.tensor_scalar(out=g_bf, in0=g_bf, scalar1=0.0, scalar2=0.5, op0=ALU.is_ge, op1=ALU.subtract)
+            if i == S_ABS_TILES[-1]:
+                nc.tensor.matmul(tot_ps[:, 0:4], lhsT=ones_f[:], rhs=part_s[:], start=True, stop=True)
+
+        r_o = const.tile([P, 1], F32, name="r_o")
+        nc.vector.tensor_reduce(out=r_o[:], in_=tot_ps[:, 0:4], axis=AX.X, op=ALU.add)
+        r_pe = const.tile([P, 1], F32, name="r_pe")
+        nc.vector.tensor_reduce(out=r_pe[:], in_=sum_ps[:], axis=AX.X, op=ALU.add)
+        mean = const.tile([P, 1], F32, name="mean")
+        nc.vector.tensor_scalar(out=mean[:], in0=r_pe[:], scalar1=r_o[:, 0:1], scalar2=1.0 / N_W, op0=ALU.add, op1=ALU.mult)
+        scale = const.tile([P, 1], F32, name="scale")
+        nc.vector.tensor_scalar(out=scale[:], in0=mean[:], scalar1=1e-5, scalar2=1000.0, op0=ALU.max, op1=ALU.min)
+        thr = const.tile([P, 1], F32, name="thr")
+        nc.vector.tensor_scalar(out=thr[:], in0=scale[:], scalar1=2.0 / 3.0, scalar2=None, op0=ALU.mult)
+        s2 = const.tile([P, 1], F32, name="s2")
+        nc.vector.tensor_scalar(out=s2[:], in0=scale[:], scalar1=2.0, scalar2=None, op0=ALU.mult)
+
+        for mt in range(N_MT):
+            xn = nat.tile([P, D_IN], BF16, tag="nat", name="xn%d" % mt)
+            nc.sync.dma_start(out=xn[:], in_=xf[P * mt : P * (mt + 1), :])
+            xg = xgp.tile([P, 2048], BF16, tag="xg", name="xg%d" % mt, align_bytes=64)
+            xw = xg[:].bitcast(F32).rearrange("p (c o u) -> p c o u", c=4, u=2)
+            transpose_tile(xn, xw, 0, 128, False)
+            nc.vector.quantize_mx(
+                out=x_codes[:, 512 * mt : 512 * (mt + 1)].bitcast(FP8X4),
+                scales=x_scales[:, 512 * mt : 512 * (mt + 1)],
+                in_=xg[:],
+            )
+        nc.sync.dma_start(out=bias_bc[:], in_=bias.partition_broadcast(P))
+
+        for j in range(N_J):
+            acc = [psum.tile([P, 512], F32, tag="b%d" % m, name="acc%d_%d" % (j, m)) for m in range(N_MT)]
+            for c in range(N_C):
+                a_c = a_t[j][:, 2048 * c : 2048 * (c + 1)]
+                g_c = g_t[j][:, 2048 * c : 2048 * (c + 1)]
+                nc.vector.tensor_scalar(out=a_c, in0=a_c, scalar1=thr[:, 0:1], scalar2=s2[:, 0:1], op0=ALU.is_gt, op1=ALU.mult)
+                nc.vector.tensor_tensor(out=g_c, in0=a_c, in1=g_c, op=ALU.mult)
+                wsl = slice(2048 * c + 512 * j, 2048 * c + 512 * (j + 1))
+                nc.vector.quantize_mx(out=w_codes[:, wsl].bitcast(FP8X4), scales=w_scales[:, wsl], in_=g_c)
+                for m in range(N_MT):
+                    xsl = slice(512 * m + 128 * c, 512 * m + 128 * (c + 1))
+                    nc.tensor.matmul_mx(
+                        out=acc[m][:],
+                        lhsT=x_codes[:, xsl].bitcast(FP8X4),
+                        lhsT_scale=x_scales[:, xsl],
+                        rhs=w_codes[:, wsl].bitcast(FP8X4),
+                        rhs_scale=w_scales[:, wsl],
+                        start=(c == 0),
+                        stop=(c == N_C - 1),
+                    )
+            for m in range(N_MT):
+                ob = osp.tile([P, 512], F32, tag="ob", name="ob%d_%d" % (j, m))
+                nc.vector.tensor_tensor(out=ob[:], in0=acc[m][:], in1=bias_bc[:, 512 * j : 512 * (j + 1)], op=ALU.add)
+                nc.sync.dma_start(out=of[P * m : P * (m + 1), 512 * j : 512 * (j + 1)], in_=ob[:])

@@ -1,8 +1,6 @@
 from contextlib import ExitStack
 
-import concourse.bass as bass
 import concourse.mybir as mybir
-import concourse.tile as tile
 from concourse.masks import make_identity
 
 F32 = mybir.dt.float32
@@ -22,11 +20,14 @@ D_OUT = 2048
 N_W = D_OUT * D_IN
 FLOPS = 2 * M_ROWS * D_IN * D_OUT
 
-N_OT = D_OUT // P
-N_MT = M_ROWS // P
-N_C = D_IN // 512
-N_J = D_OUT // 512
-S_ABS_TILES = (0, 1, 2, 3)
+N_OT = 16
+S_ABS_TILES = (1, 4, 7, 10, 13)
+X_ORDER = (4, 5, 6, 7, 0, 1, 2, 3)
+N_XG = 4
+N_NAT = 5
+LAG_A = 1
+LAG_S = 3
+LAG_G = 4
 
 
 def tile_bitnetlinear_kernel(tc, x, weight, bias, out):
@@ -34,45 +35,70 @@ def tile_bitnetlinear_kernel(tc, x, weight, bias, out):
     xf = x.flatten_outer_dims()
     of = out.flatten_outer_dims()
     with ExitStack() as ctx:
+        ctx.enter_context(tc.manual_schedule())
         const = ctx.enter_context(tc.tile_pool(name="const", bufs=1))
         keep = ctx.enter_context(tc.tile_pool(name="keep", bufs=1))
-        nat = ctx.enter_context(tc.tile_pool(name="nat", bufs=5))
-        xgp = ctx.enter_context(tc.tile_pool(name="xgp", bufs=2))
-        osp = ctx.enter_context(tc.tile_pool(name="osp", bufs=4))
+        gpool = ctx.enter_context(tc.tile_pool(name="gpool", bufs=4))
+        apool = ctx.enter_context(tc.tile_pool(name="apool", bufs=4))
+        nat = ctx.enter_context(tc.tile_pool(name="nat", bufs=N_NAT))
+        xgp = ctx.enter_context(tc.tile_pool(name="xgp", bufs=N_XG))
         psum = ctx.enter_context(tc.psum_pool(name="psum", bufs=1))
+
+        load_list = [("w", i) for i in range(N_OT)] + [("x", m) for m in X_ORDER]
+        nat_tiles = {}
+        st = {"load": 0, "bank": 0}
+
+        def load_next():
+            k = st["load"]
+            if k >= len(load_list):
+                return
+            st["load"] = k + 1
+            kind, idx = load_list[k]
+            t = nat.tile([P, D_IN], BF16, tag="nat", name="nat_%s%d" % (kind, idx))
+            src = weight if kind == "w" else xf
+            nc.sync.dma_start(out=t[:], in_=src[P * idx : P * (idx + 1), :])
+            nat_tiles[(kind, idx)] = t
+
+        for k in range(N_NAT):
+            load_next()
 
         ident = const.tile([P, P], F32, name="ident")
         make_identity(nc, ident[:])
+        ident_bf = const.tile([P, P], BF16, name="ident_bf")
+        make_identity(nc, ident_bf[:])
         ones_bf = const.tile([P, P], BF16, name="ones_bf")
         nc.vector.memset(ones_bf[:], 1.0)
         ones_f = const.tile([P, P], F32, name="ones_f")
         nc.vector.memset(ones_f[:], 1.0)
-        part_s = const.tile([P, 4], F32, name="part_s")
+        brow = const.tile([P, P], BF16, name="brow")
+        nc.vector.memset(brow[:], 0.0)
         junk = const.tile([P, 1], F32, name="junk")
         nc.vector.memset(junk[:], 0.0)
+        nc.scalar.dma_start(out=brow[0:16, :], in_=bias.rearrange("(i p) -> i p", p=P))
         junk2 = const.tile([P, 1], F32, name="junk2")
         nc.scalar.activation(out=junk2[:], in_=junk[:], func=ACT.Abs)
+        part_s = const.tile([P, 8], F32, name="part_s")
+        nc.vector.memset(part_s[:], 0.0)
+        bias_col = const.tile([P, 16], F32, name="bias_col")
         bias_bc = const.tile([P, D_OUT], BF16, name="bias_bc")
 
-        g_t = [keep.tile([P, 8192], BF16, name="g%d" % j, align_bytes=64) for j in range(N_J)]
-        a_t = [keep.tile([P, 8192], BF16, name="a%d" % j, align_bytes=64) for j in range(N_J)]
-        w_codes = keep.tile([P, N_C * D_OUT], U32, name="w_codes", align_bytes=64)
-        w_scales = keep.tile([P, N_C * D_OUT], U8, name="w_scales", align_bytes=64)
-        x_codes = keep.tile([P, N_MT * 512], U32, name="x_codes", align_bytes=64)
-        x_scales = keep.tile([P, N_MT * 512], U8, name="x_scales", align_bytes=64)
+        w_codes = keep.tile([P, 4 * D_OUT], U32, name="w_codes", align_bytes=64)
+        w_scales = keep.tile([P, 4 * D_OUT], U8, name="w_scales", align_bytes=64)
+        x_codes = keep.tile([P, 4 * M_ROWS], U32, name="x_codes", align_bytes=64)
+        x_scales = keep.tile([P, 4 * M_ROWS], U8, name="x_scales", align_bytes=64)
+        g_t = [gpool.tile([P, 8192], BF16, tag="g", name="g%d" % j, align_bytes=64) for j in range(4)]
+        a_t = [apool.tile([P, 8192], BF16, tag="a", name="a%d" % j, align_bytes=64) for j in range(4)]
 
         sum_ps = psum.tile([P, 512], F32, tag="b6", name="sum_ps")
-        tot_ps = psum.tile([P, 512], F32, tag="b7", name="tot_ps")
+        bt_ps = psum.tile([P, P], BF16, tag="b7", name="bt_ps")
 
-        state = {"bank": 0}
-
-        def transpose_tile(src, dst_words, col0, ncols_total, evac_v):
-            sv = src[:].bitcast(F32)
+        def transposes(kind, idx, nbanks):
+            sv = nat_tiles[(kind, idx)][:].bitcast(F32)
+            tiles = []
             for b in range(2):
-                bank = state["bank"] % 6
-                idx = state["bank"]
-                state["bank"] = idx + 1
-                tb = psum.tile([P, 512], F32, tag="b%d" % bank, name="tp%d" % idx)
+                n = st["bank"]
+                st["bank"] = n + 1
+                tb = psum.tile([P, 512], F32, tag="b%d" % (n % nbanks), name="tp%d" % n)
                 for q in range(4):
                     c = 2 * b + q // 2
                     u = q % 2
@@ -81,44 +107,82 @@ def tile_bitnetlinear_kernel(tc, x, weight, bias, out):
                         sv[:, 256 * c + 128 * u : 256 * c + 128 * u + 128],
                         ident[:],
                     )
-                src_ap = tb[:].rearrange("p (c u o) -> p c o u", c=2, u=2)
-                dst_ap = dst_words[:, 2 * b : 2 * b + 2, col0 : col0 + 128, :]
-                if evac_v and idx % 3 == 2:
-                    nc.vector.tensor_copy(out=dst_ap, in_=src_ap)
-                else:
-                    nc.scalar.copy(out=dst_ap, in_=src_ap)
+                tiles.append(tb)
+            return tiles
 
-        pe_tiles = [i for i in range(N_OT) if i not in S_ABS_TILES]
-        for i in range(N_OT):
+        def bank_view(tb):
+            return tb[:].rearrange("p (c u o) -> p c o u", c=2, u=2)
+
+        def w_tile(i):
             j = i // 4
             r = i % 4
-            wn = nat.tile([P, D_IN], BF16, tag="nat", name="wn%d" % i)
-            nc.sync.dma_start(out=wn[:], in_=weight[P * i : P * (i + 1), :])
+            tbs = transposes("w", i, 6)
             gw = g_t[j][:].bitcast(F32).rearrange("p (c o u) -> p c o u", c=4, u=2)
-            transpose_tile(wn, gw, 128 * r, 512, True)
-            g_bf = g_t[j][:].rearrange("p (c e) -> p c e", c=4)[:, :, 512 * r : 512 * (r + 1)]
-            a_bf = a_t[j][:].rearrange("p (c e) -> p c e", c=4)[:, :, 512 * r : 512 * (r + 1)]
+            nc.scalar.copy(out=gw[:, 0:2, 128 * r : 128 * (r + 1), :], in_=bank_view(tbs[0]))
+            nc.vector.tensor_copy(out=gw[:, 2:4, 128 * r : 128 * (r + 1), :], in_=bank_view(tbs[1]))
+
+        def views(t, i, dt, width):
+            r = i % 4
+            v = t[i // 4][:]
+            if dt is not None:
+                v = v.bitcast(dt)
+            return v.rearrange("p (c e) -> p c e", c=4)[:, :, width * r : width * (r + 1)]
+
+        def abs_tile(i):
             if i in S_ABS_TILES:
                 k = S_ABS_TILES.index(i)
-                nc.scalar.activation(out=a_bf, in_=g_bf, func=ACT.Abs, accum_out=part_s[:, k : k + 1])
+                nc.scalar.activation(
+                    out=views(a_t, i, None, 512), in_=views(g_t, i, None, 512), func=ACT.Abs,
+                    accum_out=part_s[:, k : k + 1],
+                )
             else:
-                g_i = g_t[j][:].bitcast(I32).rearrange("p (c e) -> p c e", c=4)[:, :, 256 * r : 256 * (r + 1)]
-                a_i = a_t[j][:].bitcast(I32).rearrange("p (c e) -> p c e", c=4)[:, :, 256 * r : 256 * (r + 1)]
-                nc.vector.tensor_scalar(out=a_i, in0=g_i, scalar1=0x7FFF7FFF, scalar2=None, op0=ALU.bitwise_and)
-                for c in range(N_C):
-                    nc.tensor.matmul(
-                        sum_ps[:],
-                        lhsT=ones_bf[:],
-                        rhs=a_t[j][:, 2048 * c + 512 * r : 2048 * c + 512 * (r + 1)],
-                        start=(i == pe_tiles[0] and c == 0),
-                        stop=(i == pe_tiles[-1] and c == N_C - 1),
-                    )
-            nc.vector.tensor_scalar(out=g_bf, in0=g_bf, scalar1=0.0, scalar2=0.5, op0=ALU.is_ge, op1=ALU.subtract)
-            if i == S_ABS_TILES[-1]:
-                nc.tensor.matmul(tot_ps[:, 0:4], lhsT=ones_f[:], rhs=part_s[:], start=True, stop=True)
+                nc.vector.tensor_scalar(
+                    out=views(a_t, i, I32, 256), in0=views(g_t, i, I32, 256),
+                    scalar1=0x7FFF7FFF, scalar2=None, op0=ALU.bitwise_and,
+                )
 
+        pe_tiles = [i for i in range(N_OT) if i not in S_ABS_TILES]
+
+        def sum_tile(i):
+            if i in S_ABS_TILES:
+                return
+            j = i // 4
+            r = i % 4
+            for c in range(4):
+                nc.tensor.matmul(
+                    sum_ps[:],
+                    lhsT=ones_bf[:],
+                    rhs=a_t[j][:, 2048 * c + 512 * r : 2048 * c + 512 * (r + 1)],
+                    start=(i == pe_tiles[0] and c == 0),
+                    stop=(i == pe_tiles[-1] and c == 3),
+                )
+
+        def sign_tile_v(i):
+            if i >= 8:
+                return
+            gv = views(g_t, i, None, 512)
+            nc.vector.tensor_scalar(out=gv, in0=gv, scalar1=0.0, scalar2=0.5, op0=ALU.is_ge, op1=ALU.subtract)
+
+        tot_ps = None
         r_o = const.tile([P, 1], F32, name="r_o")
-        nc.vector.tensor_reduce(out=r_o[:], in_=tot_ps[:, 0:4], axis=AX.X, op=ALU.add)
+        for i in range(N_OT + LAG_G):
+            if i < N_OT:
+                w_tile(i)
+                load_next()
+            if i == 2:
+                nc.tensor.transpose(bt_ps[:], brow[:], ident_bf[:])
+                nc.vector.tensor_copy(out=bias_col[:], in_=bt_ps[:, 0:16])
+            if 0 <= i - LAG_A < N_OT:
+                abs_tile(i - LAG_A)
+            if 0 <= i - LAG_S < N_OT:
+                sum_tile(i - LAG_S)
+            if 0 <= i - LAG_G < N_OT:
+                sign_tile_v(i - LAG_G)
+            if i == 17:
+                tot_ps = psum.tile([P, 512], F32, tag="b7", name="tot_ps")
+                nc.tensor.matmul(tot_ps[:, 0:6], lhsT=ones_f[:], rhs=part_s[:, 0:6], start=True, stop=True)
+                nc.vector.tensor_reduce(out=r_o[:], in_=tot_ps[:, 0:6], axis=AX.X, op=ALU.add)
+
         r_pe = const.tile([P, 1], F32, name="r_pe")
         nc.vector.tensor_reduce(out=r_pe[:], in_=sum_ps[:], axis=AX.X, op=ALU.add)
         mean = const.tile([P, 1], F32, name="mean")
@@ -130,40 +194,220 @@ def tile_bitnetlinear_kernel(tc, x, weight, bias, out):
         s2 = const.tile([P, 1], F32, name="s2")
         nc.vector.tensor_scalar(out=s2[:], in0=scale[:], scalar1=2.0, scalar2=None, op0=ALU.mult)
 
-        for mt in range(N_MT):
-            xn = nat.tile([P, D_IN], BF16, tag="nat", name="xn%d" % mt)
-            nc.sync.dma_start(out=xn[:], in_=xf[P * mt : P * (mt + 1), :])
-            xg = xgp.tile([P, 2048], BF16, tag="xg", name="xg%d" % mt, align_bytes=64)
-            xw = xg[:].bitcast(F32).rearrange("p (c o u) -> p c o u", c=4, u=2)
-            transpose_tile(xn, xw, 0, 128, False)
-            nc.vector.quantize_mx(
-                out=x_codes[:, 512 * mt : 512 * (mt + 1)].bitcast(FP8X4),
-                scales=x_scales[:, 512 * mt : 512 * (mt + 1)],
-                in_=xg[:],
-            )
-        nc.sync.dma_start(out=bias_bc[:], in_=bias.partition_broadcast(P))
+        xg_tiles = {}
 
-        for j in range(N_J):
-            acc = [psum.tile([P, 512], F32, tag="b%d" % m, name="acc%d_%d" % (j, m)) for m in range(N_MT)]
-            for c in range(N_C):
-                a_c = a_t[j][:, 2048 * c : 2048 * (c + 1)]
-                g_c = g_t[j][:, 2048 * c : 2048 * (c + 1)]
-                nc.vector.tensor_scalar(out=a_c, in0=a_c, scalar1=thr[:, 0:1], scalar2=s2[:, 0:1], op0=ALU.is_gt, op1=ALU.mult)
-                nc.vector.tensor_tensor(out=g_c, in0=a_c, in1=g_c, op=ALU.mult)
-                wsl = slice(2048 * c + 512 * j, 2048 * c + 512 * (j + 1))
-                nc.vector.quantize_mx(out=w_codes[:, wsl].bitcast(FP8X4), scales=w_scales[:, wsl], in_=g_c)
-                for m in range(N_MT):
-                    xsl = slice(512 * m + 128 * c, 512 * m + 128 * (c + 1))
-                    nc.tensor.matmul_mx(
-                        out=acc[m][:],
-                        lhsT=x_codes[:, xsl].bitcast(FP8X4),
-                        lhsT_scale=x_scales[:, xsl],
-                        rhs=w_codes[:, wsl].bitcast(FP8X4),
-                        rhs_scale=w_scales[:, wsl],
-                        start=(c == 0),
-                        stop=(c == N_C - 1),
+        def x_tile(pos):
+            m = X_ORDER[pos]
+            tbs = transposes("x", m, 6 if pos < 4 else 4)
+            xg = xgp.tile([P, 2048], BF16, tag="xg", name="xg%d" % m, align_bytes=64)
+            xw = xg[:].bitcast(F32).rearrange("p (c o u) -> p c o u", c=4, u=2)
+            for b in range(2):
+                nc.scalar.copy(out=xw[:, 2 * b : 2 * b + 2, :, :], in_=bank_view(tbs[b]))
+            xg_tiles[m] = xg
+            load_next()
+            if pos == 7:
+                nc.sync.dma_start(out=bias_bc[:], in_=bias.partition_broadcast(P))
+
+        def x_quant(m):
+            for c in range(4):
+                sl = slice(1024 * c + 128 * m, 1024 * c + 128 * (m + 1))
+                nc.vector.quantize_mx(
+                    out=x_codes[:, sl].bitcast(FP8X4), scales=x_scales[:, sl],
+                    in_=xg_tiles[m][:, 512 * c : 512 * (c + 1)],
+                )
+
+        def chunk(t, n):
+            return t[n // 4][:, 2048 * (n % 4) : 2048 * (n % 4 + 1)]
+
+        def m_op(n):
+            sc = s2 if n < 8 else scale
+            nc.vector.tensor_scalar(
+                out=chunk(a_t, n), in0=chunk(a_t, n), scalar1=thr[:, 0:1], scalar2=sc[:, 0:1],
+                op0=ALU.is_gt, op1=ALU.mult,
+            )
+
+        def tt_op(n):
+            nc.vector.tensor_tensor(out=chunk(g_t, n), in0=chunk(a_t, n), in1=chunk(g_t, n), op=ALU.mult)
+
+        def w_slice(n):
+            return slice(2048 * (n % 4) + 512 * (n // 4), 2048 * (n % 4) + 512 * (n // 4 + 1))
+
+        def q_op(n):
+            nc.vector.quantize_mx(
+                out=w_codes[:, w_slice(n)].bitcast(FP8X4), scales=w_scales[:, w_slice(n)], in_=chunk(g_t, n)
+            )
+
+        def sign_chunk_s(n):
+            nc.scalar.activation(out=chunk(g_t, n), in_=chunk(g_t, n), func=ACT.Sign)
+
+        acc_n = {}
+        acc_t = {}
+        to_t = {}
+        ot_t = {}
+        ob_t = {}
+
+        def alloc_n(j):
+            for m in range(4):
+                acc_n[(j, m)] = psum.tile([P, 512], F32, tag="b%d" % m, name="accn%d_%d" % (j, m))
+
+        def alloc_t(j):
+            for r in range(4):
+                acc_t[(j, r)] = psum.tile([P, 512], F32, tag="b%d" % (4 + r), name="acct%d_%d" % (j, r))
+
+        def pass_n(n, m):
+            j = n // 4
+            c = n % 4
+            xs = slice(1024 * c + 128 * m, 1024 * c + 128 * (m + 1))
+            nc.tensor.matmul_mx(
+                out=acc_n[(j, m)][:],
+                lhsT=x_codes[:, xs].bitcast(FP8X4), lhsT_scale=x_scales[:, xs],
+                rhs=w_codes[:, w_slice(n)].bitcast(FP8X4), rhs_scale=w_scales[:, w_slice(n)],
+                start=(c == 0), stop=(c == 3),
+            )
+
+        def pass_t(n):
+            j = n // 4
+            c = n % 4
+            xs = slice(1024 * c + 512, 1024 * c + 1024)
+            for r in range(4):
+                ws = slice(2048 * c + 512 * j + 128 * r, 2048 * c + 512 * j + 128 * (r + 1))
+                nc.tensor.matmul_mx(
+                    out=acc_t[(j, r)][:],
+                    lhsT=w_codes[:, ws].bitcast(FP8X4), lhsT_scale=w_scales[:, ws],
+                    rhs=x_codes[:, xs].bitcast(FP8X4), rhs_scale=x_scales[:, xs],
+                    start=(c == 0), stop=(c == 3),
+                )
+
+        def store(j, m):
+            nc.sync.dma_start(
+                out=of[P * m : P * (m + 1), 512 * j : 512 * (j + 1)], in_=ob_t[j][:, 512 * m : 512 * (m + 1)]
+            )
+
+        def r6(j, m):
+            if j not in ob_t:
+                ob_t[j] = apool.tile([P, 4096], F32, tag="a", name="ob%d" % j, align_bytes=64)
+            nc.vector.tensor_tensor(
+                out=ob_t[j][:, 512 * m : 512 * (m + 1)], in0=acc_n[(j, m)][:],
+                in1=bias_bc[:, 512 * j : 512 * (j + 1)], op=ALU.add,
+            )
+            store(j, m)
+
+        def ev1(j):
+            ot_t[j] = gpool.tile([P, 2048], F32, tag="g", name="ot%d" % j, align_bytes=64)
+            for r in range(4):
+                nc.scalar.activation(
+                    out=ot_t[j][:, 512 * r : 512 * (r + 1)], in_=acc_t[(j, r)][:], func=ACT.Identity,
+                    bias=bias_col[:, 4 * j + r : 4 * j + r + 1], scale=1.0,
+                )
+
+        def t_out(j):
+            for q in range(4):
+                to = psum.tile([P, 512], F32, tag="b%d" % (4 + q), name="to%d_%d" % (j, q))
+                for r in range(4):
+                    nc.tensor.transpose(
+                        to[:, 128 * r : 128 * (r + 1)], ot_t[j][:, 512 * r + 128 * q : 512 * r + 128 * (q + 1)], ident[:]
                     )
-            for m in range(N_MT):
-                ob = osp.tile([P, 512], F32, tag="ob", name="ob%d_%d" % (j, m))
-                nc.vector.tensor_tensor(out=ob[:], in0=acc[m][:], in1=bias_bc[:, 512 * j : 512 * (j + 1)], op=ALU.add)
-                nc.sync.dma_start(out=of[P * m : P * (m + 1), 512 * j : 512 * (j + 1)], in_=ob[:])
+                to_t[(j, q)] = to
+
+        def ev2(j, q, on_vector):
+            dst = ob_t[j][:, 512 * (4 + q) : 512 * (5 + q)]
+            if on_vector:
+                nc.vector.tensor_copy(out=dst, in_=to_t[(j, q)][:])
+            else:
+                nc.scalar.copy(out=dst, in_=to_t[(j, q)][:])
+            store(j, 4 + q)
+
+        ph = {"xt": 0, "xq": 0, "at": False, "an": False, "ev1": False}
+        x_done = set()
+        q_done = set()
+        emitted = set()
+        while ph["xt"] < N_XG:
+            x_tile(ph["xt"])
+            ph["xt"] = ph["xt"] + 1
+
+        def flush0():
+            for k in range(4):
+                if k not in q_done:
+                    continue
+                if (
+                    ("T", k) not in emitted
+                    and all(m in x_done for m in (4, 5, 6, 7))
+                    and (k == 0 or ("T", k - 1) in emitted)
+                ):
+                    if not ph["at"]:
+                        alloc_t(0)
+                        ph["at"] = True
+                    pass_t(k)
+                    emitted.add(("T", k))
+                for m in range(4):
+                    if (
+                        ph["xt"] >= 8
+                        and ("N", k, m) not in emitted
+                        and m in x_done
+                        and (k == 0 or ("N", k - 1, m) in emitted)
+                    ):
+                        if not ph["an"]:
+                            alloc_n(0)
+                            ph["an"] = True
+                        pass_n(k, m)
+                        emitted.add(("N", k, m))
+            if not ph["ev1"] and ("T", 3) in emitted:
+                ev1(0)
+                ph["ev1"] = True
+
+        def do_xq(count):
+            for rep in range(count):
+                if ph["xq"] >= 8:
+                    return
+                m = X_ORDER[ph["xq"]]
+                ph["xq"] = ph["xq"] + 1
+                x_quant(m)
+                x_done.add(m)
+                if ph["xt"] < 8:
+                    x_tile(ph["xt"])
+                    ph["xt"] = ph["xt"] + 1
+                flush0()
+
+        sign_at = {2: (8, 9, 10, 11), 6: (12, 13), 10: (14, 15)}
+        for n in range(17):
+            if 1 <= n <= 4:
+                do_xq(2)
+            if n < 16:
+                m_op(n)
+                tt_op(n)
+            if n >= 1:
+                q_op(n - 1)
+                q_done.add(n - 1)
+            if n >= 5 and n % 4 == 1:
+                for m in range(4):
+                    r6(n // 4 - 1, m)
+            if n >= 1:
+                k = n - 1
+                j = k // 4
+                c = k % 4
+                if j == 0:
+                    flush0()
+                else:
+                    if c == 0:
+                        t_out(j - 1)
+                        for q in range(4):
+                            ev2(j - 1, q, False)
+                        alloc_n(j)
+                        alloc_t(j)
+                    if k == 15:
+                        pass_t(k)
+                        for m in range(4):
+                            pass_n(k, m)
+                    else:
+                        for m in range(4):
+                            pass_n(k, m)
+                        pass_t(k)
+                    if c == 3:
+                        ev1(j)
+            for s_n in sign_at.get(n, ()):
+                sign_chunk_s(s_n)
+        for m in range(4):
+            r6(3, m)
+        t_out(3)
+        for q in range(4):
+            ev2(3, q, q % 2 == 1)

@@ -22,12 +22,15 @@ FLOPS = 2 * M_ROWS * D_IN * D_OUT
 
 N_OT = 16
 S_ABS_TILES = (1, 4, 7, 10, 13)
-X_ORDER = (4, 5, 6, 7, 0, 1, 2, 3)
+X_ORDER = (0, 1, 2, 3, 4, 5, 6, 7)
 N_XG = 4
 N_NAT = 5
 LAG_A = 1
 LAG_S = 3
 LAG_G = 4
+LAG_R = 3
+ACC_BANKS = (4, 5, 6, 7, 0, 1, 2, 3)
+X_BANKS = (0, 1, 2, 3)
 
 
 def tile_bitnetlinear_kernel(tc, x, weight, bias, out):
@@ -38,8 +41,8 @@ def tile_bitnetlinear_kernel(tc, x, weight, bias, out):
         ctx.enter_context(tc.manual_schedule())
         const = ctx.enter_context(tc.tile_pool(name="const", bufs=1))
         keep = ctx.enter_context(tc.tile_pool(name="keep", bufs=1))
-        gpool = ctx.enter_context(tc.tile_pool(name="gpool", bufs=4))
-        apool = ctx.enter_context(tc.tile_pool(name="apool", bufs=4))
+        gpool = ctx.enter_context(tc.tile_pool(name="gpool", bufs=16))
+        apool = ctx.enter_context(tc.tile_pool(name="apool", bufs=16))
         nat = ctx.enter_context(tc.tile_pool(name="nat", bufs=N_NAT))
         xgp = ctx.enter_context(tc.tile_pool(name="xgp", bufs=N_XG))
         psum = ctx.enter_context(tc.psum_pool(name="psum", bufs=1))
@@ -64,41 +67,34 @@ def tile_bitnetlinear_kernel(tc, x, weight, bias, out):
 
         ident = const.tile([P, P], F32, name="ident")
         make_identity(nc, ident[:])
-        ident_bf = const.tile([P, P], BF16, name="ident_bf")
-        make_identity(nc, ident_bf[:])
         ones_bf = const.tile([P, P], BF16, name="ones_bf")
         nc.vector.memset(ones_bf[:], 1.0)
         ones_f = const.tile([P, P], F32, name="ones_f")
         nc.vector.memset(ones_f[:], 1.0)
-        brow = const.tile([P, P], BF16, name="brow")
-        nc.vector.memset(brow[:], 0.0)
         junk = const.tile([P, 1], F32, name="junk")
         nc.vector.memset(junk[:], 0.0)
-        nc.scalar.dma_start(out=brow[0:16, :], in_=bias.rearrange("(i p) -> i p", p=P))
         junk2 = const.tile([P, 1], F32, name="junk2")
         nc.scalar.activation(out=junk2[:], in_=junk[:], func=ACT.Abs)
         part_s = const.tile([P, 8], F32, name="part_s")
         nc.vector.memset(part_s[:], 0.0)
-        bias_col = const.tile([P, 16], F32, name="bias_col")
         bias_bc = const.tile([P, D_OUT], BF16, name="bias_bc")
 
         w_codes = keep.tile([P, 4 * D_OUT], U32, name="w_codes", align_bytes=64)
         w_scales = keep.tile([P, 4 * D_OUT], U8, name="w_scales", align_bytes=64)
         x_codes = keep.tile([P, 4 * M_ROWS], U32, name="x_codes", align_bytes=64)
         x_scales = keep.tile([P, 4 * M_ROWS], U8, name="x_scales", align_bytes=64)
-        g_t = [gpool.tile([P, 8192], BF16, tag="g", name="g%d" % j, align_bytes=64) for j in range(4)]
-        a_t = [apool.tile([P, 8192], BF16, tag="a", name="a%d" % j, align_bytes=64) for j in range(4)]
+        g_t = [gpool.tile([P, 2048], BF16, tag="g", name="g%d" % i, align_bytes=64) for i in range(N_OT)]
+        a_t = [apool.tile([P, 2048], BF16, tag="a", name="a%d" % i, align_bytes=64) for i in range(N_OT)]
 
         sum_ps = psum.tile([P, 512], F32, tag="b6", name="sum_ps")
-        bt_ps = psum.tile([P, P], BF16, tag="b7", name="bt_ps")
 
-        def transposes(kind, idx, nbanks):
+        def transposes(kind, idx, banks):
             sv = nat_tiles[(kind, idx)][:].bitcast(F32)
             tiles = []
             for b in range(2):
                 n = st["bank"]
                 st["bank"] = n + 1
-                tb = psum.tile([P, 512], F32, tag="b%d" % (n % nbanks), name="tp%d" % n)
+                tb = psum.tile([P, 512], F32, tag="b%d" % banks[n % len(banks)], name="tp%d" % n)
                 for q in range(4):
                     c = 2 * b + q // 2
                     u = q % 2
@@ -113,31 +109,21 @@ def tile_bitnetlinear_kernel(tc, x, weight, bias, out):
         def bank_view(tb):
             return tb[:].rearrange("p (c u o) -> p c o u", c=2, u=2)
 
-        def w_tile(i):
-            j = i // 4
-            r = i % 4
-            tbs = transposes("w", i, 6)
-            gw = g_t[j][:].bitcast(F32).rearrange("p (c o u) -> p c o u", c=4, u=2)
-            nc.scalar.copy(out=gw[:, 0:2, 128 * r : 128 * (r + 1), :], in_=bank_view(tbs[0]))
-            nc.vector.tensor_copy(out=gw[:, 2:4, 128 * r : 128 * (r + 1), :], in_=bank_view(tbs[1]))
+        def half_view(t, b):
+            return t[:].bitcast(F32)[:, 512 * b : 512 * (b + 1)].rearrange("p (c o u) -> p c o u", c=2, u=2)
 
-        def views(t, i, dt, width):
-            r = i % 4
-            v = t[i // 4][:]
-            if dt is not None:
-                v = v.bitcast(dt)
-            return v.rearrange("p (c e) -> p c e", c=4)[:, :, width * r : width * (r + 1)]
+        def w_tile(i):
+            tbs = transposes("w", i, (0, 1, 2, 3, 4, 5))
+            nc.scalar.copy(out=half_view(g_t[i], 0), in_=bank_view(tbs[0]))
+            nc.vector.tensor_copy(out=half_view(g_t[i], 1), in_=bank_view(tbs[1]))
 
         def abs_tile(i):
             if i in S_ABS_TILES:
                 k = S_ABS_TILES.index(i)
-                nc.scalar.activation(
-                    out=views(a_t, i, None, 512), in_=views(g_t, i, None, 512), func=ACT.Abs,
-                    accum_out=part_s[:, k : k + 1],
-                )
+                nc.scalar.activation(out=a_t[i][:], in_=g_t[i][:], func=ACT.Abs, accum_out=part_s[:, k : k + 1])
             else:
                 nc.vector.tensor_scalar(
-                    out=views(a_t, i, I32, 256), in0=views(g_t, i, I32, 256),
+                    out=a_t[i][:].bitcast(I32), in0=g_t[i][:].bitcast(I32),
                     scalar1=0x7FFF7FFF, scalar2=None, op0=ALU.bitwise_and,
                 )
 
@@ -146,32 +132,24 @@ def tile_bitnetlinear_kernel(tc, x, weight, bias, out):
         def sum_tile(i):
             if i in S_ABS_TILES:
                 return
-            j = i // 4
-            r = i % 4
             for c in range(4):
                 nc.tensor.matmul(
-                    sum_ps[:],
-                    lhsT=ones_bf[:],
-                    rhs=a_t[j][:, 2048 * c + 512 * r : 2048 * c + 512 * (r + 1)],
-                    start=(i == pe_tiles[0] and c == 0),
-                    stop=(i == pe_tiles[-1] and c == 3),
+                    sum_ps[:], lhsT=ones_bf[:], rhs=a_t[i][:, 512 * c : 512 * (c + 1)],
+                    start=(i == pe_tiles[0] and c == 0), stop=(i == pe_tiles[-1] and c == 3),
                 )
 
         def sign_tile_v(i):
             if i >= 8:
                 return
-            gv = views(g_t, i, None, 512)
-            nc.vector.tensor_scalar(out=gv, in0=gv, scalar1=0.0, scalar2=0.5, op0=ALU.is_ge, op1=ALU.subtract)
+            nc.vector.tensor_scalar(
+                out=g_t[i][:], in0=g_t[i][:], scalar1=0.0, scalar2=0.5, op0=ALU.is_ge, op1=ALU.subtract
+            )
 
-        tot_ps = None
         r_o = const.tile([P, 1], F32, name="r_o")
         for i in range(N_OT + LAG_G):
             if i < N_OT:
                 w_tile(i)
                 load_next()
-            if i == 2:
-                nc.tensor.transpose(bt_ps[:], brow[:], ident_bf[:])
-                nc.vector.tensor_copy(out=bias_col[:], in_=bt_ps[:, 0:16])
             if 0 <= i - LAG_A < N_OT:
                 abs_tile(i - LAG_A)
             if 0 <= i - LAG_S < N_OT:
@@ -198,126 +176,71 @@ def tile_bitnetlinear_kernel(tc, x, weight, bias, out):
 
         def x_tile(pos):
             m = X_ORDER[pos]
-            tbs = transposes("x", m, 6 if pos < 4 else 4)
+            tbs = transposes("x", m, X_BANKS)
             xg = xgp.tile([P, 2048], BF16, tag="xg", name="xg%d" % m, align_bytes=64)
-            xw = xg[:].bitcast(F32).rearrange("p (c o u) -> p c o u", c=4, u=2)
             for b in range(2):
-                nc.scalar.copy(out=xw[:, 2 * b : 2 * b + 2, :, :], in_=bank_view(tbs[b]))
+                nc.scalar.copy(out=half_view(xg, b), in_=bank_view(tbs[b]))
             xg_tiles[m] = xg
             load_next()
             if pos == 7:
                 nc.sync.dma_start(out=bias_bc[:], in_=bias.partition_broadcast(P))
+                for i in range(8, N_OT):
+                    nc.scalar.activation(out=g_t[i][:], in_=g_t[i][:], func=ACT.Sign)
 
         def x_quant(m):
-            for c in range(4):
-                sl = slice(1024 * c + 128 * m, 1024 * c + 128 * (m + 1))
-                nc.vector.quantize_mx(
-                    out=x_codes[:, sl].bitcast(FP8X4), scales=x_scales[:, sl],
-                    in_=xg_tiles[m][:, 512 * c : 512 * (c + 1)],
-                )
+            sl = slice(512 * m, 512 * (m + 1))
+            nc.vector.quantize_mx(out=x_codes[:, sl].bitcast(FP8X4), scales=x_scales[:, sl], in_=xg_tiles[m][:])
 
-        def chunk(t, n):
-            return t[n // 4][:, 2048 * (n % 4) : 2048 * (n % 4 + 1)]
-
-        def m_op(n):
-            sc = s2 if n < 8 else scale
+        def m_op(i):
+            sc = s2 if i < 8 else scale
             nc.vector.tensor_scalar(
-                out=chunk(a_t, n), in0=chunk(a_t, n), scalar1=thr[:, 0:1], scalar2=sc[:, 0:1],
-                op0=ALU.is_gt, op1=ALU.mult,
+                out=a_t[i][:], in0=a_t[i][:], scalar1=thr[:, 0:1], scalar2=sc[:, 0:1], op0=ALU.is_gt, op1=ALU.mult
             )
 
-        def tt_op(n):
-            nc.vector.tensor_tensor(out=chunk(g_t, n), in0=chunk(a_t, n), in1=chunk(g_t, n), op=ALU.mult)
+        def tt_op(i):
+            nc.vector.tensor_tensor(out=g_t[i][:], in0=a_t[i][:], in1=g_t[i][:], op=ALU.mult)
 
-        def w_slice(n):
-            return slice(2048 * (n % 4) + 512 * (n // 4), 2048 * (n % 4) + 512 * (n // 4 + 1))
+        def q_op(i):
+            sl = slice(512 * i, 512 * (i + 1))
+            nc.vector.quantize_mx(out=w_codes[:, sl].bitcast(FP8X4), scales=w_scales[:, sl], in_=g_t[i][:])
 
-        def q_op(n):
-            nc.vector.quantize_mx(
-                out=w_codes[:, w_slice(n)].bitcast(FP8X4), scales=w_scales[:, w_slice(n)], in_=chunk(g_t, n)
-            )
-
-        def sign_chunk_s(n):
-            nc.scalar.activation(out=chunk(g_t, n), in_=chunk(g_t, n), func=ACT.Sign)
-
-        acc_n = {}
-        acc_t = {}
-        to_t = {}
-        ot_t = {}
+        acc = {}
         ob_t = {}
+        ph = {"xt": 0, "xq": 0, "pb": 0, "r6": 0}
 
-        def alloc_n(j):
-            for m in range(4):
-                acc_n[(j, m)] = psum.tile([P, 512], F32, tag="b%d" % m, name="accn%d_%d" % (j, m))
+        def bank_ok():
+            return not (ACC_BANKS[ph["pb"] % 8] in X_BANKS and ph["xt"] < 8)
 
-        def alloc_t(j):
-            for r in range(4):
-                acc_t[(j, r)] = psum.tile([P, 512], F32, tag="b%d" % (4 + r), name="acct%d_%d" % (j, r))
-
-        def pass_n(n, m):
-            j = n // 4
-            c = n % 4
-            xs = slice(1024 * c + 128 * m, 1024 * c + 128 * (m + 1))
-            nc.tensor.matmul_mx(
-                out=acc_n[(j, m)][:],
-                lhsT=x_codes[:, xs].bitcast(FP8X4), lhsT_scale=x_scales[:, xs],
-                rhs=w_codes[:, w_slice(n)].bitcast(FP8X4), rhs_scale=w_scales[:, w_slice(n)],
-                start=(c == 0), stop=(c == 3),
-            )
-
-        def pass_t(n):
-            j = n // 4
-            c = n % 4
-            xs = slice(1024 * c + 512, 1024 * c + 1024)
-            for r in range(4):
-                ws = slice(2048 * c + 512 * j + 128 * r, 2048 * c + 512 * j + 128 * (r + 1))
+        def group(i, m):
+            h = m // 4
+            if (i, h) not in acc:
+                bank = ACC_BANKS[ph["pb"] % 8]
+                ph["pb"] = ph["pb"] + 1
+                acc[(i, h)] = psum.tile([P, 512], F32, tag="b%d" % bank, name="acc%d_%d" % (i, h))
+            for c in range(4):
+                xs = slice(512 * m + 128 * c, 512 * m + 128 * (c + 1))
+                ws = slice(512 * i + 128 * c, 512 * i + 128 * (c + 1))
                 nc.tensor.matmul_mx(
-                    out=acc_t[(j, r)][:],
-                    lhsT=w_codes[:, ws].bitcast(FP8X4), lhsT_scale=w_scales[:, ws],
-                    rhs=x_codes[:, xs].bitcast(FP8X4), rhs_scale=x_scales[:, xs],
+                    out=acc[(i, h)][:, 128 * (m % 4) : 128 * (m % 4 + 1)],
+                    lhsT=x_codes[:, xs].bitcast(FP8X4), lhsT_scale=x_scales[:, xs],
+                    rhs=w_codes[:, ws].bitcast(FP8X4), rhs_scale=w_scales[:, ws],
                     start=(c == 0), stop=(c == 3),
                 )
 
-        def store(j, m):
-            nc.sync.dma_start(
-                out=of[P * m : P * (m + 1), 512 * j : 512 * (j + 1)], in_=ob_t[j][:, 512 * m : 512 * (m + 1)]
-            )
-
-        def r6(j, m):
-            if j not in ob_t:
-                ob_t[j] = apool.tile([P, 4096], F32, tag="a", name="ob%d" % j, align_bytes=64)
+        def r6(i, h):
+            if i not in ob_t:
+                ob_t[i] = apool.tile([P, 1024], F32, tag="a", name="ob%d" % i, align_bytes=64)
+            dst = ob_t[i][:, 512 * h : 512 * (h + 1)].rearrange("p (t o) -> p t o", t=4)
             nc.vector.tensor_tensor(
-                out=ob_t[j][:, 512 * m : 512 * (m + 1)], in0=acc_n[(j, m)][:],
-                in1=bias_bc[:, 512 * j : 512 * (j + 1)], op=ALU.add,
+                out=dst,
+                in0=acc[(i, h)][:].rearrange("p (t o) -> p t o", t=4),
+                in1=bias_bc[:, P * i : P * (i + 1)].unsqueeze(1).to_broadcast([P, 4, P]),
+                op=ALU.add,
             )
-            store(j, m)
+            nc.sync.dma_start(
+                out=of[512 * h : 512 * (h + 1), P * i : P * (i + 1)].rearrange("(t p) o -> p t o", p=P), in_=dst
+            )
 
-        def ev1(j):
-            ot_t[j] = gpool.tile([P, 2048], F32, tag="g", name="ot%d" % j, align_bytes=64)
-            for r in range(4):
-                nc.scalar.activation(
-                    out=ot_t[j][:, 512 * r : 512 * (r + 1)], in_=acc_t[(j, r)][:], func=ACT.Identity,
-                    bias=bias_col[:, 4 * j + r : 4 * j + r + 1], scale=1.0,
-                )
-
-        def t_out(j):
-            for q in range(4):
-                to = psum.tile([P, 512], F32, tag="b%d" % (4 + q), name="to%d_%d" % (j, q))
-                for r in range(4):
-                    nc.tensor.transpose(
-                        to[:, 128 * r : 128 * (r + 1)], ot_t[j][:, 512 * r + 128 * q : 512 * r + 128 * (q + 1)], ident[:]
-                    )
-                to_t[(j, q)] = to
-
-        def ev2(j, q, on_vector):
-            dst = ob_t[j][:, 512 * (4 + q) : 512 * (5 + q)]
-            if on_vector:
-                nc.vector.tensor_copy(out=dst, in_=to_t[(j, q)][:])
-            else:
-                nc.scalar.copy(out=dst, in_=to_t[(j, q)][:])
-            store(j, 4 + q)
-
-        ph = {"xt": 0, "xq": 0, "at": False, "an": False, "ev1": False}
         x_done = set()
         q_done = set()
         emitted = set()
@@ -325,35 +248,22 @@ def tile_bitnetlinear_kernel(tc, x, weight, bias, out):
             x_tile(ph["xt"])
             ph["xt"] = ph["xt"] + 1
 
-        def flush0():
-            for k in range(4):
-                if k not in q_done:
+        def flush():
+            for i in range(N_OT):
+                if i not in q_done:
+                    return
+                if ("done", i) in emitted:
                     continue
-                if (
-                    ("T", k) not in emitted
-                    and all(m in x_done for m in (4, 5, 6, 7))
-                    and (k == 0 or ("T", k - 1) in emitted)
-                ):
-                    if not ph["at"]:
-                        alloc_t(0)
-                        ph["at"] = True
-                    pass_t(k)
-                    emitted.add(("T", k))
-                for m in range(4):
-                    if (
-                        ph["xt"] >= 8
-                        and ("N", k, m) not in emitted
-                        and m in x_done
-                        and (k == 0 or ("N", k - 1, m) in emitted)
-                    ):
-                        if not ph["an"]:
-                            alloc_n(0)
-                            ph["an"] = True
-                        pass_n(k, m)
-                        emitted.add(("N", k, m))
-            if not ph["ev1"] and ("T", 3) in emitted:
-                ev1(0)
-                ph["ev1"] = True
+                for m in range(8):
+                    if (i, m) in emitted:
+                        continue
+                    if m not in x_done:
+                        return
+                    if (i, m // 4) not in acc and not bank_ok():
+                        return
+                    group(i, m)
+                    emitted.add((i, m))
+                emitted.add(("done", i))
 
         def do_xq(count):
             for rep in range(count):
@@ -366,48 +276,23 @@ def tile_bitnetlinear_kernel(tc, x, weight, bias, out):
                 if ph["xt"] < 8:
                     x_tile(ph["xt"])
                     ph["xt"] = ph["xt"] + 1
-                flush0()
+                flush()
 
-        sign_at = {2: (8, 9, 10, 11), 6: (12, 13), 10: (14, 15)}
-        for n in range(17):
+        r6_queue = []
+        for n in range(N_OT + LAG_R + 1):
             if 1 <= n <= 4:
                 do_xq(2)
-            if n < 16:
+            if n < N_OT:
                 m_op(n)
                 tt_op(n)
-            if n >= 1:
+            if 1 <= n <= N_OT:
                 q_op(n - 1)
                 q_done.add(n - 1)
-            if n >= 5 and n % 4 == 1:
-                for m in range(4):
-                    r6(n // 4 - 1, m)
-            if n >= 1:
-                k = n - 1
-                j = k // 4
-                c = k % 4
-                if j == 0:
-                    flush0()
-                else:
-                    if c == 0:
-                        t_out(j - 1)
-                        for q in range(4):
-                            ev2(j - 1, q, False)
-                        alloc_n(j)
-                        alloc_t(j)
-                    if k == 15:
-                        pass_t(k)
-                        for m in range(4):
-                            pass_n(k, m)
-                    else:
-                        for m in range(4):
-                            pass_n(k, m)
-                        pass_t(k)
-                    if c == 3:
-                        ev1(j)
-            for s_n in sign_at.get(n, ()):
-                sign_chunk_s(s_n)
-        for m in range(4):
-            r6(3, m)
-        t_out(3)
-        for q in range(4):
-            ev2(3, q, q % 2 == 1)
+                flush()
+            if 0 <= n - LAG_R < N_OT:
+                r6_queue.append((n - LAG_R, 0))
+                r6_queue.append((n - LAG_R, 1))
+            while ph["r6"] < len(r6_queue) and ("done", r6_queue[ph["r6"]][0]) in emitted:
+                i, h = r6_queue[ph["r6"]]
+                ph["r6"] = ph["r6"] + 1
+                r6(i, h)

@@ -21,7 +21,8 @@ N_W = D_OUT * D_IN
 FLOPS = 2 * M_ROWS * D_IN * D_OUT
 
 N_OT = 16
-S_ABS_TILES = (1, 4, 7, 10, 13)
+S_ABS_TILES = (0, 2, 4, 7, 9, 11, 14)
+S_M_TILES = (11, 12, 13, 14, 15)
 X_ORDER = (0, 1, 2, 3, 4, 5, 6, 7)
 N_XG = 4
 N_NAT = 5
@@ -114,7 +115,10 @@ def tile_bitnetlinear_kernel(tc, x, weight, bias, out):
 
         def w_tile(i):
             tbs = transposes("w", i, (0, 1, 2, 3, 4, 5))
-            nc.scalar.copy(out=half_view(g_t[i], 0), in_=bank_view(tbs[0]))
+            if i in S_ABS_TILES:
+                nc.vector.tensor_copy(out=half_view(g_t[i], 0), in_=bank_view(tbs[0]))
+            else:
+                nc.scalar.copy(out=half_view(g_t[i], 0), in_=bank_view(tbs[0]))
             nc.vector.tensor_copy(out=half_view(g_t[i], 1), in_=bank_view(tbs[1]))
 
         def abs_tile(i):
@@ -158,19 +162,29 @@ def tile_bitnetlinear_kernel(tc, x, weight, bias, out):
                 sign_tile_v(i - LAG_G)
             if i == 17:
                 tot_ps = psum.tile([P, 512], F32, tag="b7", name="tot_ps")
-                nc.tensor.matmul(tot_ps[:, 0:6], lhsT=ones_f[:], rhs=part_s[:, 0:6], start=True, stop=True)
-                nc.vector.tensor_reduce(out=r_o[:], in_=tot_ps[:, 0:6], axis=AX.X, op=ALU.add)
+                nc.tensor.matmul(tot_ps[:, 0:8], lhsT=ones_f[:], rhs=part_s[:, 0:8], start=True, stop=True)
+                nc.vector.tensor_reduce(out=r_o[:], in_=tot_ps[:, 0:8], axis=AX.X, op=ALU.add)
 
         r_pe = const.tile([P, 1], F32, name="r_pe")
         nc.vector.tensor_reduce(out=r_pe[:], in_=sum_ps[:], axis=AX.X, op=ALU.add)
-        mean = const.tile([P, 1], F32, name="mean")
-        nc.vector.tensor_scalar(out=mean[:], in0=r_pe[:], scalar1=r_o[:, 0:1], scalar2=1.0 / N_W, op0=ALU.add, op1=ALU.mult)
-        scale = const.tile([P, 1], F32, name="scale")
-        nc.vector.tensor_scalar(out=scale[:], in0=mean[:], scalar1=1e-5, scalar2=1000.0, op0=ALU.max, op1=ALU.min)
-        thr = const.tile([P, 1], F32, name="thr")
-        nc.vector.tensor_scalar(out=thr[:], in0=scale[:], scalar1=2.0 / 3.0, scalar2=None, op0=ALU.mult)
-        s2 = const.tile([P, 1], F32, name="s2")
-        nc.vector.tensor_scalar(out=s2[:], in0=scale[:], scalar1=2.0, scalar2=None, op0=ALU.mult)
+        def clipped(name, factor):
+            raw = const.tile([P, 1], F32, name=name + "_raw")
+            nc.vector.tensor_scalar(
+                out=raw[:], in0=r_pe[:], scalar1=r_o[:, 0:1], scalar2=factor / N_W, op0=ALU.add, op1=ALU.mult
+            )
+            return raw
+
+        def clip_op(name, raw, factor):
+            res = const.tile([P, 1], F32, name=name)
+            nc.vector.tensor_scalar(
+                out=res[:], in0=raw[:], scalar1=factor * 1e-5, scalar2=factor * 1000.0, op0=ALU.max, op1=ALU.min
+            )
+            return res
+
+        thr_raw = clipped("thr", 2.0 / 3.0)
+        s2_raw = clipped("s2", 2.0)
+        thr = clip_op("thr", thr_raw, 2.0 / 3.0)
+        s2 = clip_op("s2", s2_raw, 2.0)
 
         xg_tiles = {}
 
@@ -186,13 +200,22 @@ def tile_bitnetlinear_kernel(tc, x, weight, bias, out):
                 nc.sync.dma_start(out=bias_bc[:], in_=bias.partition_broadcast(P))
                 for i in range(8, N_OT):
                     nc.scalar.activation(out=g_t[i][:], in_=g_t[i][:], func=ACT.Sign)
+                for i in S_M_TILES:
+                    nc.scalar.activation(
+                        out=a_t[i][:], in_=a_t[i][:], func=ACT.Sign, bias=late["neg_thr"][:, 0:1], scale=1.0
+                    )
+                    nc.scalar.activation(out=a_t[i][:], in_=a_t[i][:], func=ACT.Relu, scale=late["scale"][:, 0:1])
 
         def x_quant(m):
             sl = slice(512 * m, 512 * (m + 1))
             nc.vector.quantize_mx(out=x_codes[:, sl].bitcast(FP8X4), scales=x_scales[:, sl], in_=xg_tiles[m][:])
 
+        late = {}
+
         def m_op(i):
-            sc = s2 if i < 8 else scale
+            if i in S_M_TILES:
+                return
+            sc = s2 if i < 8 else late["scale"]
             nc.vector.tensor_scalar(
                 out=a_t[i][:], in0=a_t[i][:], scalar1=thr[:, 0:1], scalar2=sc[:, 0:1], op0=ALU.is_gt, op1=ALU.mult
             )
@@ -282,9 +305,16 @@ def tile_bitnetlinear_kernel(tc, x, weight, bias, out):
         for n in range(N_OT + LAG_R + 1):
             if 1 <= n <= 4:
                 do_xq(2)
+            if n == 0:
+                m_op(0)
+            if n + 1 < N_OT:
+                m_op(n + 1)
             if n < N_OT:
-                m_op(n)
                 tt_op(n)
+            if n == 0:
+                late["scale"] = clip_op("scale", clipped("scale", 1.0), 1.0)
+                late["neg_thr"] = const.tile([P, 1], F32, name="neg_thr")
+                nc.vector.tensor_scalar(out=late["neg_thr"][:], in0=thr[:], scalar1=-1.0, scalar2=None, op0=ALU.mult)
             if 1 <= n <= N_OT:
                 q_op(n - 1)
                 q_done.add(n - 1)

@@ -21,17 +21,26 @@ N_W = D_OUT * D_IN
 FLOPS = 2 * M_ROWS * D_IN * D_OUT
 
 N_OT = 16
-S_ABS_TILES = (0, 2, 4, 7, 9, 11, 14)
-S_M_TILES = (11, 12, 13, 14, 15)
-X_ORDER = (0, 1, 2, 3, 4, 5, 6, 7)
-N_XG = 4
-N_NAT = 5
-LAG_A = 1
-LAG_S = 3
-LAG_G = 4
-LAG_R = 3
-ACC_BANKS = (4, 5, 6, 7, 0, 1, 2, 3)
+N_XT = 8
+GROUPS = ((0, 1), (2, 3), (4, 5), (6, 7), (8, 9), (10, 11), (12, 13), (14,), (15,))
+S_ABS_TILES = (0, 2, 4, 6, 8, 10, 12, 14)
+N_EARLY = 10
+S_COPY = ()
+COPY_LAG = 1
+SUM_LAG = 1
+V_P1_UNITS = (0, 1, 2, 3)
+S_P3_UNITS = ()
+LATE_WITH = {2: (10, 11), 3: (12, 13), 4: (14, 15)}
+XQ_FIRST = 1
+FILL_FROM = 3
+R6_KEEP = 2
+N_NAT = 14
+ACC_BANKS = (4, 5, 6, 7, 2, 3)
+LATE_BANKS = (0, 1)
 X_BANKS = (0, 1, 2, 3)
+W_BANKS = (0, 1, 2, 3, 4, 5)
+EDGE = (2.0 - 2.0**-8) * (1.0 - 2.0**-21)
+SIGN_AND_TWO = -0x3FFF4000
 
 
 def tile_bitnetlinear_kernel(tc, x, weight, bias, out):
@@ -43,12 +52,12 @@ def tile_bitnetlinear_kernel(tc, x, weight, bias, out):
         const = ctx.enter_context(tc.tile_pool(name="const", bufs=1))
         keep = ctx.enter_context(tc.tile_pool(name="keep", bufs=1))
         gpool = ctx.enter_context(tc.tile_pool(name="gpool", bufs=16))
-        apool = ctx.enter_context(tc.tile_pool(name="apool", bufs=16))
+        apool = ctx.enter_context(tc.tile_pool(name="apool", bufs=8))
+        obp = ctx.enter_context(tc.tile_pool(name="obp", bufs=6))
         nat = ctx.enter_context(tc.tile_pool(name="nat", bufs=N_NAT))
-        xgp = ctx.enter_context(tc.tile_pool(name="xgp", bufs=N_XG))
         psum = ctx.enter_context(tc.psum_pool(name="psum", bufs=1))
 
-        load_list = [("w", i) for i in range(N_OT)] + [("x", m) for m in X_ORDER]
+        load_list = [("w", i) for i in range(N_OT)] + [("x", m) for m in range(N_XT)]
         nat_tiles = {}
         st = {"load": 0, "bank": 0}
 
@@ -60,7 +69,10 @@ def tile_bitnetlinear_kernel(tc, x, weight, bias, out):
             kind, idx = load_list[k]
             t = nat.tile([P, D_IN], BF16, tag="nat", name="nat_%s%d" % (kind, idx))
             src = weight if kind == "w" else xf
-            nc.sync.dma_start(out=t[:], in_=src[P * idx : P * (idx + 1), :])
+            parts = 2 if (kind, idx) == ("w", N_OT - 1) else 1
+            for h in range(parts):
+                sl = slice(D_IN // parts * h, D_IN // parts * (h + 1))
+                nc.sync.dma_start(out=t[:, sl], in_=src[P * idx : P * (idx + 1), sl])
             nat_tiles[(kind, idx)] = t
 
         for k in range(N_NAT):
@@ -69,9 +81,10 @@ def tile_bitnetlinear_kernel(tc, x, weight, bias, out):
         ident = const.tile([P, P], F32, name="ident")
         make_identity(nc, ident[:])
         ones_bf = const.tile([P, P], BF16, name="ones_bf")
-        nc.vector.memset(ones_bf[:], 1.0)
+        nc.vector.memset(ones_bf[:], 1.0 / N_W)
         ones_f = const.tile([P, P], F32, name="ones_f")
-        nc.vector.memset(ones_f[:], 1.0)
+        nc.vector.memset(ones_f[:], 1.0 / N_W)
+        s_abs = const.tile([P, D_IN], BF16, name="s_abs")
         junk = const.tile([P, 1], F32, name="junk")
         nc.vector.memset(junk[:], 0.0)
         junk2 = const.tile([P, 1], F32, name="junk2")
@@ -85,244 +98,296 @@ def tile_bitnetlinear_kernel(tc, x, weight, bias, out):
         x_codes = keep.tile([P, 4 * M_ROWS], U32, name="x_codes", align_bytes=64)
         x_scales = keep.tile([P, 4 * M_ROWS], U8, name="x_scales", align_bytes=64)
         g_t = [gpool.tile([P, 2048], BF16, tag="g", name="g%d" % i, align_bytes=64) for i in range(N_OT)]
-        a_t = [apool.tile([P, 2048], BF16, tag="a", name="a%d" % i, align_bytes=64) for i in range(N_OT)]
 
         sum_ps = psum.tile([P, 512], F32, tag="b6", name="sum_ps")
 
-        def transposes(kind, idx, banks):
+        group_of = {}
+        first_unit = []
+        unit_group = []
+        for g, tiles in enumerate(GROUPS):
+            first_unit.append(len(unit_group))
+            for pos, i in enumerate(tiles):
+                group_of[i] = (g, pos)
+                unit_group.append(g)
+        N_U = len(unit_group)
+
+        def unit_tiles(u):
+            return GROUPS[unit_group[u]]
+
+        def half_transposes(kind, idx, b, bank):
             sv = nat_tiles[(kind, idx)][:].bitcast(F32)
-            tiles = []
-            for b in range(2):
-                n = st["bank"]
-                st["bank"] = n + 1
-                tb = psum.tile([P, 512], F32, tag="b%d" % banks[n % len(banks)], name="tp%d" % n)
-                for q in range(4):
-                    c = 2 * b + q // 2
-                    u = q % 2
-                    nc.tensor.transpose(
-                        tb[:, 128 * q : 128 * (q + 1)],
-                        sv[:, 256 * c + 128 * u : 256 * c + 128 * u + 128],
-                        ident[:],
-                    )
-                tiles.append(tb)
-            return tiles
+            st["bank"] = st["bank"] + 1
+            tb = psum.tile([P, 512], F32, tag="b%d" % bank, name="tp%d" % st["bank"])
+            for q in range(4):
+                lo = 512 * b + 128 * q
+                nc.tensor.transpose(tb[:, 128 * q : 128 * (q + 1)], sv[:, lo : lo + 128], ident[:])
+            return tb
 
         def bank_view(tb):
             return tb[:].rearrange("p (c u o) -> p c o u", c=2, u=2)
 
-        def half_view(t, b):
-            return t[:].bitcast(F32)[:, 512 * b : 512 * (b + 1)].rearrange("p (c o u) -> p c o u", c=2, u=2)
+        def w_unit_part(i, b):
+            g, pos = group_of[i]
+            if len(GROUPS[g]) == 2:
+                return first_unit[g] + b, 0, 2, 128 * pos, 256
+            return first_unit[g], 2 * b, 4, 0, 128
 
-        def w_tile(i):
-            tbs = transposes("w", i, (0, 1, 2, 3, 4, 5))
-            if i in S_ABS_TILES:
-                nc.vector.tensor_copy(out=half_view(g_t[i], 0), in_=bank_view(tbs[0]))
-            else:
-                nc.scalar.copy(out=half_view(g_t[i], 0), in_=bank_view(tbs[0]))
-            nc.vector.tensor_copy(out=half_view(g_t[i], 1), in_=bank_view(tbs[1]))
+        def w_dst(i, b):
+            u, c0, cs, o0, ow = w_unit_part(i, b)
+            v = g_t[u][:].bitcast(F32).rearrange("p (c o u) -> p c o u", c=cs, u=2)
+            return v[:, c0 : c0 + 2, o0 : o0 + 128, :]
 
-        def abs_tile(i):
-            if i in S_ABS_TILES:
-                k = S_ABS_TILES.index(i)
-                nc.scalar.activation(out=a_t[i][:], in_=g_t[i][:], func=ACT.Abs, accum_out=part_s[:, k : k + 1])
-            else:
-                nc.vector.tensor_scalar(
-                    out=a_t[i][:].bitcast(I32), in0=g_t[i][:].bitcast(I32),
-                    scalar1=0x7FFF7FFF, scalar2=None, op0=ALU.bitwise_and,
-                )
+        w_bank = {}
+        wb = {"n": 0}
+
+        def w_transposes(i):
+            for b in range(2):
+                w_bank[(i, b)] = half_transposes("w", i, b, W_BANKS[wb["n"] % len(W_BANKS)])
+                wb["n"] = wb["n"] + 1
+
+        def w_copy(i):
+            for b in range(2):
+                if (i, b) in S_COPY:
+                    nc.scalar.copy(out=w_dst(i, b), in_=bank_view(w_bank[(i, b)]))
+                else:
+                    nc.vector.tensor_copy(out=w_dst(i, b), in_=bank_view(w_bank[(i, b)]))
 
         pe_tiles = [i for i in range(N_OT) if i not in S_ABS_TILES]
+        abs_t = {}
+
+        def abs_tile(i):
+            src = nat_tiles[("w", i)]
+            if i in S_ABS_TILES:
+                k = S_ABS_TILES.index(i)
+                nc.scalar.activation(out=s_abs[:], in_=src[:], func=ACT.Abs, accum_out=part_s[:, k : k + 1])
+                return
+            a = apool.tile([P, 2048], BF16, tag="a", name="a%d" % i, align_bytes=64)
+            abs_t[i] = a
+            parts = 2 if i == N_OT - 1 else 1
+            for h in range(parts):
+                sl = slice(D_IN // parts * h, D_IN // parts * (h + 1))
+                nc.vector.tensor_scalar(
+                    out=a[:, sl].bitcast(I32), in0=src[:, sl].bitcast(I32),
+                    scalar1=0x7FFF7FFF, scalar2=None, op0=ALU.bitwise_and,
+                )
 
         def sum_tile(i):
             if i in S_ABS_TILES:
                 return
-            for c in range(4):
+            a = abs_t[i]
+            for c in range(8):
                 nc.tensor.matmul(
-                    sum_ps[:], lhsT=ones_bf[:], rhs=a_t[i][:, 512 * c : 512 * (c + 1)],
-                    start=(i == pe_tiles[0] and c == 0), stop=(i == pe_tiles[-1] and c == 3),
+                    sum_ps[:, 0:256], lhsT=ones_bf[:], rhs=a[:, 256 * c : 256 * (c + 1)],
+                    start=(i == pe_tiles[0] and c == 0), stop=(i == pe_tiles[-1] and c == 7),
                 )
 
-        def sign_tile_v(i):
-            if i >= 8:
-                return
-            nc.vector.tensor_scalar(
-                out=g_t[i][:], in0=g_t[i][:], scalar1=0.0, scalar2=0.5, op0=ALU.is_ge, op1=ALU.subtract
-            )
-
-        r_o = const.tile([P, 1], F32, name="r_o")
-        for i in range(N_OT + LAG_G):
-            if i < N_OT:
-                w_tile(i)
+        for i in range(N_OT):
+            if 0 <= i - COPY_LAG < N_EARLY - 1:
+                w_copy(i - COPY_LAG)
+            abs_tile(i)
+            if i < N_EARLY:
+                w_transposes(i)
+            if i >= SUM_LAG:
+                sum_tile(i - SUM_LAG)
+            if i >= 1:
                 load_next()
-            if 0 <= i - LAG_A < N_OT:
-                abs_tile(i - LAG_A)
-            if 0 <= i - LAG_S < N_OT:
-                sum_tile(i - LAG_S)
-            if 0 <= i - LAG_G < N_OT:
-                sign_tile_v(i - LAG_G)
-            if i == 17:
-                tot_ps = psum.tile([P, 512], F32, tag="b7", name="tot_ps")
-                nc.tensor.matmul(tot_ps[:, 0:8], lhsT=ones_f[:], rhs=part_s[:, 0:8], start=True, stop=True)
-                nc.vector.tensor_reduce(out=r_o[:], in_=tot_ps[:, 0:8], axis=AX.X, op=ALU.add)
+        for i in range(N_OT - SUM_LAG, N_OT):
+            sum_tile(i)
+        nc.tensor.matmul(sum_ps[:, 256:264], lhsT=ones_f[:], rhs=part_s[:, 0:8], start=True, stop=True)
+        w_copy(N_EARLY - 1)
 
-        r_pe = const.tile([P, 1], F32, name="r_pe")
-        nc.vector.tensor_reduce(out=r_pe[:], in_=sum_ps[:], axis=AX.X, op=ALU.add)
-        def clipped(name, factor):
-            raw = const.tile([P, 1], F32, name=name + "_raw")
-            nc.vector.tensor_scalar(
-                out=raw[:], in0=r_pe[:], scalar1=r_o[:, 0:1], scalar2=factor / N_W, op0=ALU.add, op1=ALU.mult
-            )
-            return raw
+        mean = const.tile([P, 1], F32, name="mean")
+        nc.vector.tensor_reduce(out=mean[:], in_=sum_ps[:, 0:264], axis=AX.X, op=ALU.add)
+        scale = const.tile([P, 1], F32, name="scale")
+        nc.vector.tensor_scalar(
+            out=scale[:], in0=mean[:], scalar1=1e-5, scalar2=1000.0, op0=ALU.max, op1=ALU.min
+        )
+        inv = const.tile([P, 1], F32, name="inv")
+        nc.vector.reciprocal(out=inv[:], in_=scale[:])
+        up = const.tile([P, 1], F32, name="up")
+        half = const.tile([P, 1], F32, name="half")
 
-        def clip_op(name, raw, factor):
-            res = const.tile([P, 1], F32, name=name)
-            nc.vector.tensor_scalar(
-                out=res[:], in0=raw[:], scalar1=factor * 1e-5, scalar2=factor * 1000.0, op0=ALU.max, op1=ALU.min
-            )
-            return res
-
-        thr_raw = clipped("thr", 2.0 / 3.0)
-        s2_raw = clipped("s2", 2.0)
-        thr = clip_op("thr", thr_raw, 2.0 / 3.0)
-        s2 = clip_op("s2", s2_raw, 2.0)
+        def late_scalars():
+            nc.vector.tensor_scalar(out=up[:], in0=inv[:], scalar1=1.5 * EDGE, scalar2=None, op0=ALU.mult)
+            nc.vector.tensor_scalar(out=half[:], in0=scale[:], scalar1=0.5, scalar2=None, op0=ALU.mult)
 
         xg_tiles = {}
+        xb = {"n": 0}
 
-        def x_tile(pos):
-            m = X_ORDER[pos]
-            tbs = transposes("x", m, X_BANKS)
-            xg = xgp.tile([P, 2048], BF16, tag="xg", name="xg%d" % m, align_bytes=64)
+        def x_tile(m):
+            xg = apool.tile([P, 2048], BF16, tag="a", name="xg%d" % m, align_bytes=64)
+            xv = xg[:].bitcast(F32).rearrange("p (c o u) -> p c o u", c=4, u=2)
             for b in range(2):
-                nc.scalar.copy(out=half_view(xg, b), in_=bank_view(tbs[b]))
+                tb = half_transposes("x", m, b, X_BANKS[xb["n"] % len(X_BANKS)])
+                xb["n"] = xb["n"] + 1
+                nc.scalar.copy(out=xv[:, 2 * b : 2 * b + 2, :, :], in_=bank_view(tb))
             xg_tiles[m] = xg
             load_next()
-            if pos == 7:
+            if m == N_XT - 1:
                 nc.sync.dma_start(out=bias_bc[:], in_=bias.partition_broadcast(P))
-                for i in range(8, N_OT):
-                    nc.scalar.activation(out=g_t[i][:], in_=g_t[i][:], func=ACT.Sign)
-                for i in S_M_TILES:
-                    nc.scalar.activation(
-                        out=a_t[i][:], in_=a_t[i][:], func=ACT.Sign, bias=late["neg_thr"][:, 0:1], scale=1.0
-                    )
-                    nc.scalar.activation(out=a_t[i][:], in_=a_t[i][:], func=ACT.Relu, scale=late["scale"][:, 0:1])
 
         def x_quant(m):
             sl = slice(512 * m, 512 * (m + 1))
             nc.vector.quantize_mx(out=x_codes[:, sl].bitcast(FP8X4), scales=x_scales[:, sl], in_=xg_tiles[m][:])
 
-        late = {}
+        def late_unit(u):
+            tiles = unit_tiles(u)
+            for k in range(2):
+                i, b = (tiles[k], u - first_unit[unit_group[u]]) if len(tiles) == 2 else (tiles[0], k)
+                tb = half_transposes("w", i, b, LATE_BANKS[k])
+                uu, c0, cs, o0, ow = w_unit_part(i, b)
+                for c in range(2):
+                    lo = 4 * ((c0 + c) * ow + o0)
+                    nc.scalar.activation(
+                        out=g_t[u][:, lo : lo + 512].rearrange("p (o u e) -> p o u e", u=2, e=2),
+                        in_=tb[:, 256 * c : 256 * (c + 1)].bitcast(BF16).rearrange("p (u o e) -> p o u e", u=2, e=2),
+                        func=ACT.Copy, scale=up[:, 0:1],
+                    )
 
-        def m_op(i):
-            if i in S_M_TILES:
-                return
-            sc = s2 if i < 8 else late["scale"]
+        def p1(u):
+            if u in V_P1_UNITS:
+                nc.vector.tensor_scalar(
+                    out=g_t[u][:], in0=g_t[u][:], scalar1=inv[:, 0:1], scalar2=1.5 * EDGE, op0=ALU.mult, op1=ALU.mult
+                )
+
+        def p2(u):
             nc.vector.tensor_scalar(
-                out=a_t[i][:], in0=a_t[i][:], scalar1=thr[:, 0:1], scalar2=sc[:, 0:1], op0=ALU.is_gt, op1=ALU.mult
+                out=g_t[u][:].bitcast(I32), in0=g_t[u][:].bitcast(I32),
+                scalar1=SIGN_AND_TWO, scalar2=None, op0=ALU.bitwise_and,
             )
 
-        def tt_op(i):
-            nc.vector.tensor_tensor(out=g_t[i][:], in0=a_t[i][:], in1=g_t[i][:], op=ALU.mult)
+        def p3(u):
+            if u in S_P3_UNITS:
+                nc.scalar.activation(out=g_t[u][:], in_=g_t[u][:], func=ACT.Copy, scale=half[:, 0:1])
+            else:
+                nc.vector.tensor_scalar(out=g_t[u][:], in0=g_t[u][:], scalar1=half[:, 0:1], scalar2=None, op0=ALU.mult)
 
-        def q_op(i):
-            sl = slice(512 * i, 512 * (i + 1))
-            nc.vector.quantize_mx(out=w_codes[:, sl].bitcast(FP8X4), scales=w_scales[:, sl], in_=g_t[i][:])
+        def q_op(u):
+            sl = slice(512 * u, 512 * (u + 1))
+            nc.vector.quantize_mx(out=w_codes[:, sl].bitcast(FP8X4), scales=w_scales[:, sl], in_=g_t[u][:])
 
+        opened = []
+        stored = set()
+        closed = []
         acc = {}
-        ob_t = {}
         ph = {"xt": 0, "xq": 0, "pb": 0, "r6": 0}
 
-        def bank_ok():
-            return not (ACC_BANKS[ph["pb"] % 8] in X_BANKS and ph["xt"] < 8)
-
-        def group(i, m):
-            h = m // 4
-            if (i, h) not in acc:
-                bank = ACC_BANKS[ph["pb"] % 8]
+        def mx_group(g, m):
+            width = 128 * len(GROUPS[g])
+            per_bank = 512 // width
+            key = (g, m // per_bank)
+            if key not in acc:
+                if ph["pb"] >= len(ACC_BANKS):
+                    old = opened[ph["pb"] - len(ACC_BANKS)]
+                    while old not in stored:
+                        r6_next()
+                bank = ACC_BANKS[ph["pb"] % len(ACC_BANKS)]
                 ph["pb"] = ph["pb"] + 1
-                acc[(i, h)] = psum.tile([P, 512], F32, tag="b%d" % bank, name="acc%d_%d" % (i, h))
+                opened.append(key)
+                acc[key] = psum.tile([P, 512], F32, tag="b%d" % bank, name="acc%d_%d" % key)
+            col = width * (m % per_bank)
             for c in range(4):
                 xs = slice(512 * m + 128 * c, 512 * m + 128 * (c + 1))
-                ws = slice(512 * i + 128 * c, 512 * i + 128 * (c + 1))
+                lo = 512 * first_unit[g] + width * c
+                ws = slice(lo, lo + width)
                 nc.tensor.matmul_mx(
-                    out=acc[(i, h)][:, 128 * (m % 4) : 128 * (m % 4 + 1)],
+                    out=acc[key][:, col : col + width],
                     lhsT=x_codes[:, xs].bitcast(FP8X4), lhsT_scale=x_scales[:, xs],
                     rhs=w_codes[:, ws].bitcast(FP8X4), rhs_scale=w_scales[:, ws],
                     start=(c == 0), stop=(c == 3),
                 )
 
-        def r6(i, h):
-            if i not in ob_t:
-                ob_t[i] = apool.tile([P, 1024], F32, tag="a", name="ob%d" % i, align_bytes=64)
-            dst = ob_t[i][:, 512 * h : 512 * (h + 1)].rearrange("p (t o) -> p t o", t=4)
+        def r6(g, h):
+            width = 128 * len(GROUPS[g])
+            per_bank = 512 // width
+            o0 = P * GROUPS[g][0]
+            ob = obp.tile([P, 512], F32, tag="ob", name="ob%d_%d" % (g, h), align_bytes=64)
+            dst = ob[:].rearrange("p (t o) -> p t o", t=per_bank)
             nc.vector.tensor_tensor(
                 out=dst,
-                in0=acc[(i, h)][:].rearrange("p (t o) -> p t o", t=4),
-                in1=bias_bc[:, P * i : P * (i + 1)].unsqueeze(1).to_broadcast([P, 4, P]),
+                in0=acc[(g, h)][:].rearrange("p (t o) -> p t o", t=per_bank),
+                in1=bias_bc[:, o0 : o0 + width].unsqueeze(1).to_broadcast([P, per_bank, width]),
                 op=ALU.add,
             )
+            rows = P * per_bank
             nc.sync.dma_start(
-                out=of[512 * h : 512 * (h + 1), P * i : P * (i + 1)].rearrange("(t p) o -> p t o", p=P), in_=dst
+                out=of[rows * h : rows * (h + 1), o0 : o0 + width].rearrange("(t p) o -> p t o", p=P), in_=dst
             )
 
-        x_done = set()
-        q_done = set()
-        emitted = set()
-        while ph["xt"] < N_XG:
-            x_tile(ph["xt"])
-            ph["xt"] = ph["xt"] + 1
+        def r6_next():
+            g, h = closed[ph["r6"]]
+            ph["r6"] = ph["r6"] + 1
+            stored.add((g, h))
+            r6(g, h)
 
-        def flush():
-            for i in range(N_OT):
-                if i not in q_done:
-                    return
-                if ("done", i) in emitted:
-                    continue
-                for m in range(8):
-                    if (i, m) in emitted:
-                        continue
-                    if m not in x_done:
-                        return
-                    if (i, m // 4) not in acc and not bank_ok():
-                        return
-                    group(i, m)
-                    emitted.add((i, m))
-                emitted.add(("done", i))
+        def s_p1(u):
+            if u not in V_P1_UNITS and unit_tiles(u)[-1] < N_EARLY:
+                nc.scalar.activation(out=g_t[u][:], in_=g_t[u][:], func=ACT.Copy, scale=up[:, 0:1])
 
-        def do_xq(count):
-            for rep in range(count):
-                if ph["xq"] >= 8:
-                    return
-                m = X_ORDER[ph["xq"]]
-                ph["xq"] = ph["xq"] + 1
+        def units(g):
+            if not 0 <= g < len(GROUPS):
+                return []
+            return [first_unit[g] + k for k in range(len(GROUPS[g]))]
+
+        def mx_tokens(g, m):
+            per_bank = 4 // len(GROUPS[g])
+            mx_group(g, m)
+            if m % per_bank == per_bank - 1:
+                closed.append((g, m // per_bank))
+
+        for m in range(N_XT):
+            x_tile(m)
+        for u in units(0):
+            p1(u)
+        late_scalars()
+        for u in range(N_U):
+            s_p1(u)
+        for u in units(0):
+            p2(u)
+        for m in range(XQ_FIRST):
+            x_quant(m)
+        for u in units(0):
+            p3(u)
+        for u in units(0):
+            q_op(u)
+        fill = [(p1, u) for u in units(1)] + [(p2, u) for u in units(1)]
+        for m in range(N_XT):
+            if m >= XQ_FIRST:
                 x_quant(m)
-                x_done.add(m)
-                if ph["xt"] < 8:
-                    x_tile(ph["xt"])
-                    ph["xt"] = ph["xt"] + 1
-                flush()
-
-        r6_queue = []
-        for n in range(N_OT + LAG_R + 1):
-            if 1 <= n <= 4:
-                do_xq(2)
-            if n == 0:
-                m_op(0)
-            if n + 1 < N_OT:
-                m_op(n + 1)
-            if n < N_OT:
-                tt_op(n)
-            if n == 0:
-                late["scale"] = clip_op("scale", clipped("scale", 1.0), 1.0)
-                late["neg_thr"] = const.tile([P, 1], F32, name="neg_thr")
-                nc.vector.tensor_scalar(out=late["neg_thr"][:], in0=thr[:], scalar1=-1.0, scalar2=None, op0=ALU.mult)
-            if 1 <= n <= N_OT:
-                q_op(n - 1)
-                q_done.add(n - 1)
-                flush()
-            if 0 <= n - LAG_R < N_OT:
-                r6_queue.append((n - LAG_R, 0))
-                r6_queue.append((n - LAG_R, 1))
-            while ph["r6"] < len(r6_queue) and ("done", r6_queue[ph["r6"]][0]) in emitted:
-                i, h = r6_queue[ph["r6"]]
-                ph["r6"] = ph["r6"] + 1
-                r6(i, h)
+                if fill and m >= FILL_FROM:
+                    f, u = fill.pop(0)
+                    f(u)
+            mx_tokens(0, m)
+        for f, u in fill:
+            f(u)
+        for g in range(1, len(GROUPS)):
+            for u in units(g):
+                if u in S_P3_UNITS:
+                    p3(u)
+            before = [(p3, u) for u in units(g) if u not in S_P3_UNITS] + [(q_op, u) for u in units(g)]
+            after = [(p1, u) for u in units(g + 1) if u in V_P1_UNITS] + [(p2, u) for u in units(g + 1)]
+            n_r6 = max(0, len(closed) - ph["r6"] - R6_KEEP)
+            n_before = n_r6 // 2 if g > 1 else 0
+            k = 0
+            for f, u in before:
+                f(u)
+                if k >= 1 and n_before > 0:
+                    r6_next()
+                    n_before = n_before - 1
+                    n_r6 = n_r6 - 1
+                k = k + 1
+            late = LATE_WITH.get(g, ())
+            for m in range(N_XT):
+                if m % 4 == 0 and m // 4 < len(late):
+                    late_unit(late[m // 4])
+                mx_tokens(g, m)
+            for f, u in after:
+                f(u)
+                if n_r6 > 0:
+                    r6_next()
+                    n_r6 = n_r6 - 1
+            while n_r6 > 0:
+                r6_next()
+                n_r6 = n_r6 - 1
+        while ph["r6"] < len(closed):
+            r6_next()

@@ -23,15 +23,17 @@ FLOPS = 2 * M_ROWS * D_IN * D_OUT
 N_OT = 16
 N_XT = 8
 GROUPS = ((0, 1), (2, 3), (4, 5), (6, 7), (8, 9), (10, 11), (12, 13), (14,), (15,))
-S_ABS_TILES = (0, 2, 4, 6, 8, 10, 12, 14)
+S_HALVES = tuple((i, h) for i in (0, 2, 4, 6, 8, 10, 13,) for h in range(2)) + ()
 N_EARLY = 10
-S_COPY = ()
+S_COPY = ((2, 0), (4, 0), (6, 0), (8, 0))
 COPY_LAG = 1
 SUM_LAG = 1
 V_P1_UNITS = (0, 1, 2, 3)
-S_P3_UNITS = ()
-LATE_WITH = {2: (10, 11), 3: (12, 13), 4: (14, 15)}
+S_P3_UNITS = (12, 13)
+LATE_WITH = {2: (10,), 3: (11, 12), 4: (13, 14), 5: (15,)}
 XQ_FIRST = 1
+X_BEFORE = 4
+S_P1_AT = {}
 FILL_FROM = 3
 R6_KEEP = 2
 N_NAT = 14
@@ -152,39 +154,48 @@ def tile_bitnetlinear_kernel(tc, x, weight, bias, out):
                 else:
                     nc.vector.tensor_copy(out=w_dst(i, b), in_=bank_view(w_bank[(i, b)]))
 
-        pe_tiles = [i for i in range(N_OT) if i not in S_ABS_TILES]
         abs_t = {}
+        s_col = {"n": 0}
+        v_halves = [(i, h) for i in range(N_OT) for h in range(2) if (i, h) not in S_HALVES]
+        HALF = D_IN // 2
 
         def abs_tile(i):
             src = nat_tiles[("w", i)]
-            if i in S_ABS_TILES:
-                k = S_ABS_TILES.index(i)
-                nc.scalar.activation(out=s_abs[:], in_=src[:], func=ACT.Abs, accum_out=part_s[:, k : k + 1])
-                return
-            a = apool.tile([P, 2048], BF16, tag="a", name="a%d" % i, align_bytes=64)
-            abs_t[i] = a
-            parts = 2 if i == N_OT - 1 else 1
-            for h in range(parts):
-                sl = slice(D_IN // parts * h, D_IN // parts * (h + 1))
-                nc.vector.tensor_scalar(
-                    out=a[:, sl].bitcast(I32), in0=src[:, sl].bitcast(I32),
-                    scalar1=0x7FFF7FFF, scalar2=None, op0=ALU.bitwise_and,
-                )
+            for mine in (True, False):
+                hs = [h for h in range(2) if ((i, h) in S_HALVES) == mine]
+                spans = [(HALF * h, HALF * (h + 1)) for h in hs]
+                if len(hs) == 2 and i != N_OT - 1:
+                    spans = [(0, D_IN)]
+                for lo, hi in spans:
+                    if mine:
+                        k = s_col["n"]
+                        s_col["n"] = k + 1
+                        nc.scalar.activation(
+                            out=s_abs[:, lo:hi], in_=src[:, lo:hi], func=ACT.Abs, accum_out=part_s[:, k : k + 1]
+                        )
+                        continue
+                    if i not in abs_t:
+                        abs_t[i] = apool.tile([P, 2048], BF16, tag="a", name="a%d" % i, align_bytes=64)
+                    nc.vector.tensor_scalar(
+                        out=abs_t[i][:, lo:hi].bitcast(I32), in0=src[:, lo:hi].bitcast(I32),
+                        scalar1=0x7FFF7FFF, scalar2=None, op0=ALU.bitwise_and,
+                    )
 
         def sum_tile(i):
-            if i in S_ABS_TILES:
-                return
-            a = abs_t[i]
-            for c in range(8):
-                nc.tensor.matmul(
-                    sum_ps[:, 0:256], lhsT=ones_bf[:], rhs=a[:, 256 * c : 256 * (c + 1)],
-                    start=(i == pe_tiles[0] and c == 0), stop=(i == pe_tiles[-1] and c == 7),
-                )
+            for h in range(2):
+                if (i, h) in S_HALVES:
+                    continue
+                for c in range(4):
+                    lo = HALF * h + 256 * c
+                    nc.tensor.matmul(
+                        sum_ps[:, 0:256], lhsT=ones_bf[:], rhs=abs_t[i][:, lo : lo + 256],
+                        start=((i, h) == v_halves[0] and c == 0), stop=((i, h) == v_halves[-1] and c == 3),
+                    )
 
         for i in range(N_OT):
+            abs_tile(i)
             if 0 <= i - COPY_LAG < N_EARLY - 1:
                 w_copy(i - COPY_LAG)
-            abs_tile(i)
             if i < N_EARLY:
                 w_transposes(i)
             if i >= SUM_LAG:
@@ -324,6 +335,10 @@ def tile_bitnetlinear_kernel(tc, x, weight, bias, out):
             if u not in V_P1_UNITS and unit_tiles(u)[-1] < N_EARLY:
                 nc.scalar.activation(out=g_t[u][:], in_=g_t[u][:], func=ACT.Copy, scale=up[:, 0:1])
 
+        def p2_s(u):
+            p2(u)
+            p3(u)
+
         def units(g):
             if not 0 <= g < len(GROUPS):
                 return []
@@ -335,13 +350,18 @@ def tile_bitnetlinear_kernel(tc, x, weight, bias, out):
             if m % per_bank == per_bank - 1:
                 closed.append((g, m // per_bank))
 
-        for m in range(N_XT):
+        for m in range(X_BEFORE):
             x_tile(m)
         for u in units(0):
             p1(u)
         late_scalars()
+        for m in range(X_BEFORE, N_XT):
+            if m in S_P1_AT:
+                s_p1(S_P1_AT[m])
+            x_tile(m)
         for u in range(N_U):
-            s_p1(u)
+            if u not in S_P1_AT.values():
+                s_p1(u)
         for u in units(0):
             p2(u)
         for m in range(XQ_FIRST):
@@ -361,11 +381,10 @@ def tile_bitnetlinear_kernel(tc, x, weight, bias, out):
         for f, u in fill:
             f(u)
         for g in range(1, len(GROUPS)):
-            for u in units(g):
-                if u in S_P3_UNITS:
-                    p3(u)
             before = [(p3, u) for u in units(g) if u not in S_P3_UNITS] + [(q_op, u) for u in units(g)]
-            after = [(p1, u) for u in units(g + 1) if u in V_P1_UNITS] + [(p2, u) for u in units(g + 1)]
+            after = [(p1, u) for u in units(g + 1) if u in V_P1_UNITS]
+            after = after + [(p2, u) for u in units(g + 1) if u not in S_P3_UNITS]
+            after = after + [(p2_s, u) for u in units(g + 2) if u in S_P3_UNITS]
             n_r6 = max(0, len(closed) - ph["r6"] - R6_KEEP)
             n_before = n_r6 // 2 if g > 1 else 0
             k = 0

@@ -23,9 +23,10 @@ FLOPS = 2 * M_ROWS * D_IN * D_OUT
 N_OT = 16
 N_XT = 8
 GROUPS = ((0, 1), (2, 3), (4, 5), (6, 7), (8, 9), (10, 11), (12, 13), (14,), (15,))
-S_HALVES = tuple((i, h) for i in (0, 2, 4, 6, 8, 10, 13,) for h in range(2)) + ()
+S_HALVES = tuple((i, h) for i in (0, 2, 4, 6, 8, 10) for h in range(2)) + ((12, 0), (13, 0), (14, 0))
+N_PROMPT = 9
 N_EARLY = 10
-S_COPY = ((2, 0), (4, 0), (6, 0), (8, 0))
+S_COPY = ((8, 0), (9, 0))
 COPY_LAG = 1
 SUM_LAG = 1
 V_P1_UNITS = (0, 1, 2, 3)
@@ -36,7 +37,8 @@ X_BEFORE = 4
 S_P1_AT = {}
 FILL_FROM = 3
 R6_KEEP = 2
-N_NAT = 14
+HALVED = (15,)
+N_NAT = 7
 ACC_BANKS = (4, 5, 6, 7, 2, 3)
 LATE_BANKS = (0, 1)
 X_BANKS = (0, 1, 2, 3)
@@ -55,11 +57,11 @@ def tile_bitnetlinear_kernel(tc, x, weight, bias, out):
         keep = ctx.enter_context(tc.tile_pool(name="keep", bufs=1))
         gpool = ctx.enter_context(tc.tile_pool(name="gpool", bufs=16))
         apool = ctx.enter_context(tc.tile_pool(name="apool", bufs=8))
-        obp = ctx.enter_context(tc.tile_pool(name="obp", bufs=6))
+        obp = ctx.enter_context(tc.tile_pool(name="obp", bufs=8))
         nat = ctx.enter_context(tc.tile_pool(name="nat", bufs=N_NAT))
         psum = ctx.enter_context(tc.psum_pool(name="psum", bufs=1))
 
-        load_list = [("w", i) for i in range(N_OT)] + [("x", m) for m in range(N_XT)]
+        load_list = [("w", q) for q in range(N_OT // 2)] + [("x", q) for q in range(N_XT // 2)]
         nat_tiles = {}
         st = {"load": 0, "bank": 0}
 
@@ -68,14 +70,23 @@ def tile_bitnetlinear_kernel(tc, x, weight, bias, out):
             if k >= len(load_list):
                 return
             st["load"] = k + 1
-            kind, idx = load_list[k]
-            t = nat.tile([P, D_IN], BF16, tag="nat", name="nat_%s%d" % (kind, idx))
+            kind, q = load_list[k]
+            t = nat.tile([P, 2 * D_IN], BF16, tag="nat", name="nat_%s%d" % (kind, q))
             src = weight if kind == "w" else xf
-            parts = 2 if (kind, idx) == ("w", N_OT - 1) else 1
-            for h in range(parts):
-                sl = slice(D_IN // parts * h, D_IN // parts * (h + 1))
-                nc.sync.dma_start(out=t[:, sl], in_=src[P * idx : P * (idx + 1), sl])
-            nat_tiles[(kind, idx)] = t
+            rows = src[2 * P * q : 2 * P * (q + 1), :]
+            for j in range(2):
+                nat_tiles[(kind, 2 * q + j)] = t[:, D_IN * j : D_IN * (j + 1)]
+            if kind == "w" and q == N_OT // 2 - 1:
+                nc.sync.dma_start(out=t[:, 0:D_IN], in_=rows[0:P, :])
+                for h in range(2):
+                    lo = D_IN // 2 * h
+                    nc.sync.dma_start(out=t[:, D_IN + lo : D_IN + lo + D_IN // 2], in_=rows[P : 2 * P, lo : lo + D_IN // 2])
+            elif q == 0:
+                by_row = rows.rearrange("(p j) i -> p j i", j=2)
+                for j in range(2):
+                    nc.sync.dma_start(out=t[:, D_IN * j : D_IN * (j + 1)], in_=by_row[:, j, :])
+            else:
+                nc.sync.dma_start(out=t[:], in_=rows.rearrange("(p j) i -> p (j i)", j=2))
 
         for k in range(N_NAT):
             load_next()
@@ -91,7 +102,7 @@ def tile_bitnetlinear_kernel(tc, x, weight, bias, out):
         nc.vector.memset(junk[:], 0.0)
         junk2 = const.tile([P, 1], F32, name="junk2")
         nc.scalar.activation(out=junk2[:], in_=junk[:], func=ACT.Abs)
-        part_s = const.tile([P, 8], F32, name="part_s")
+        part_s = const.tile([P, 16], F32, name="part_s")
         nc.vector.memset(part_s[:], 0.0)
         bias_bc = const.tile([P, D_OUT], BF16, name="bias_bc")
 
@@ -117,7 +128,7 @@ def tile_bitnetlinear_kernel(tc, x, weight, bias, out):
             return GROUPS[unit_group[u]]
 
         def half_transposes(kind, idx, b, bank):
-            sv = nat_tiles[(kind, idx)][:].bitcast(F32)
+            sv = nat_tiles[(kind, idx)].bitcast(F32)
             st["bank"] = st["bank"] + 1
             tb = psum.tile([P, 512], F32, tag="b%d" % bank, name="tp%d" % st["bank"])
             for q in range(4):
@@ -164,7 +175,7 @@ def tile_bitnetlinear_kernel(tc, x, weight, bias, out):
             for mine in (True, False):
                 hs = [h for h in range(2) if ((i, h) in S_HALVES) == mine]
                 spans = [(HALF * h, HALF * (h + 1)) for h in hs]
-                if len(hs) == 2 and i != N_OT - 1:
+                if len(hs) == 2 and i not in HALVED:
                     spans = [(0, D_IN)]
                 for lo, hi in spans:
                     if mine:
@@ -194,21 +205,22 @@ def tile_bitnetlinear_kernel(tc, x, weight, bias, out):
 
         for i in range(N_OT):
             abs_tile(i)
-            if 0 <= i - COPY_LAG < N_EARLY - 1:
+            if 0 <= i - COPY_LAG < N_PROMPT:
                 w_copy(i - COPY_LAG)
             if i < N_EARLY:
                 w_transposes(i)
             if i >= SUM_LAG:
                 sum_tile(i - SUM_LAG)
-            if i >= 1:
+            if i % 2 == 1:
                 load_next()
         for i in range(N_OT - SUM_LAG, N_OT):
             sum_tile(i)
-        nc.tensor.matmul(sum_ps[:, 256:264], lhsT=ones_f[:], rhs=part_s[:, 0:8], start=True, stop=True)
-        w_copy(N_EARLY - 1)
+        nc.tensor.matmul(sum_ps[:, 256:272], lhsT=ones_f[:], rhs=part_s[:], start=True, stop=True)
+        for i in range(N_PROMPT, N_EARLY):
+            w_copy(i)
 
         mean = const.tile([P, 1], F32, name="mean")
-        nc.vector.tensor_reduce(out=mean[:], in_=sum_ps[:, 0:264], axis=AX.X, op=ALU.add)
+        nc.vector.tensor_reduce(out=mean[:], in_=sum_ps[:, 0:272], axis=AX.X, op=ALU.add)
         scale = const.tile([P, 1], F32, name="scale")
         nc.vector.tensor_scalar(
             out=scale[:], in0=mean[:], scalar1=1e-5, scalar2=1000.0, op0=ALU.max, op1=ALU.min
@@ -233,7 +245,6 @@ def tile_bitnetlinear_kernel(tc, x, weight, bias, out):
                 xb["n"] = xb["n"] + 1
                 nc.scalar.copy(out=xv[:, 2 * b : 2 * b + 2, :, :], in_=bank_view(tb))
             xg_tiles[m] = xg
-            load_next()
             if m == N_XT - 1:
                 nc.sync.dma_start(out=bias_bc[:], in_=bias.partition_broadcast(P))
 
@@ -285,7 +296,7 @@ def tile_bitnetlinear_kernel(tc, x, weight, bias, out):
 
         def mx_group(g, m):
             width = 128 * len(GROUPS[g])
-            per_bank = 512 // width
+            per_bank = 2
             key = (g, m // per_bank)
             if key not in acc:
                 if ph["pb"] >= len(ACC_BANKS):
@@ -310,19 +321,28 @@ def tile_bitnetlinear_kernel(tc, x, weight, bias, out):
 
         def r6(g, h):
             width = 128 * len(GROUPS[g])
-            per_bank = 512 // width
             o0 = P * GROUPS[g][0]
             ob = obp.tile([P, 512], F32, tag="ob", name="ob%d_%d" % (g, h), align_bytes=64)
-            dst = ob[:].rearrange("p (t o) -> p t o", t=per_bank)
-            nc.vector.tensor_tensor(
-                out=dst,
-                in0=acc[(g, h)][:].rearrange("p (t o) -> p t o", t=per_bank),
-                in1=bias_bc[:, o0 : o0 + width].unsqueeze(1).to_broadcast([P, per_bank, width]),
-                op=ALU.add,
-            )
-            rows = P * per_bank
+            flat = ob[:, 0 : 2 * width]
+            b_row = bias_bc[:, o0 : o0 + width]
+            ps = acc[(g, h)][:, 0 : 2 * width]
+            if len(GROUPS[g]) == 2:
+                nc.vector.tensor_tensor(
+                    out=flat.rearrange("p (t q j) -> p t q j", t=2, j=2),
+                    in0=ps.rearrange("p (t j q) -> p t q j", t=2, j=2),
+                    in1=b_row.rearrange("p (q j) -> p q j", j=2).unsqueeze(1).to_broadcast([P, 2, P, 2]),
+                    op=ALU.add,
+                )
+            else:
+                nc.vector.tensor_tensor(
+                    out=flat.rearrange("p (t o) -> p t o", t=2),
+                    in0=ps.rearrange("p (t o) -> p t o", t=2),
+                    in1=b_row.unsqueeze(1).to_broadcast([P, 2, width]),
+                    op=ALU.add,
+                )
             nc.sync.dma_start(
-                out=of[rows * h : rows * (h + 1), o0 : o0 + width].rearrange("(t p) o -> p t o", p=P), in_=dst
+                out=of[256 * h : 256 * (h + 1), o0 : o0 + width].rearrange("(p t) o -> p t o", t=2),
+                in_=flat.rearrange("p (t o) -> p t o", t=2),
             )
 
         def r6_next():
@@ -345,7 +365,7 @@ def tile_bitnetlinear_kernel(tc, x, weight, bias, out):
             return [first_unit[g] + k for k in range(len(GROUPS[g]))]
 
         def mx_tokens(g, m):
-            per_bank = 4 // len(GROUPS[g])
+            per_bank = 2
             mx_group(g, m)
             if m % per_bank == per_bank - 1:
                 closed.append((g, m // per_bank))

@@ -23,20 +23,20 @@ FLOPS = 2 * M_ROWS * D_IN * D_OUT
 N_OT = 16
 N_XT = 8
 GROUPS = ((0, 1), (2, 3), (4, 5), (6, 7), (8, 9), (10, 11), (12, 13), (14,), (15,))
-S_HALVES = tuple((i, h) for i in (0, 2, 4, 6, 8, 10) for h in range(2)) + ((12, 0), (13, 0), (14, 0))
-N_PROMPT = 9
+S_HALVES = tuple((i, h) for i in (0, 2, 4, 6, 8, 10, 12) for h in range(2)) + ((14, 0),)
+N_PROMPT = 8
 N_EARLY = 10
-S_COPY = ((8, 0), (9, 0))
+S_COPY = ((8, 0), (8, 1), (9, 0), (9, 1))
 COPY_LAG = 1
 SUM_LAG = 1
-V_P1_UNITS = (0, 1, 2, 3)
-S_P3_UNITS = (12, 13)
+V_P1_UNITS = (0, 1, 2, 3, 4)
+S_P3_UNITS = (13, 14, 15)
 LATE_WITH = {2: (10,), 3: (11, 12), 4: (13, 14), 5: (15,)}
-XQ_FIRST = 1
+XQ_FIRST = 0
 X_BEFORE = 4
 S_P1_AT = {}
-FILL_FROM = 3
-R6_KEEP = 2
+FILL_FROM = 2
+R6_KEEP = 3
 HALVED = (15,)
 N_NAT = 7
 ACC_BANKS = (4, 5, 6, 7, 2, 3)
@@ -97,7 +97,6 @@ def tile_bitnetlinear_kernel(tc, x, weight, bias, out):
         nc.vector.memset(ones_bf[:], 1.0 / N_W)
         ones_f = const.tile([P, P], F32, name="ones_f")
         nc.vector.memset(ones_f[:], 1.0 / N_W)
-        s_abs = const.tile([P, D_IN], BF16, name="s_abs")
         junk = const.tile([P, 1], F32, name="junk")
         nc.vector.memset(junk[:], 0.0)
         junk2 = const.tile([P, 1], F32, name="junk2")
@@ -182,7 +181,7 @@ def tile_bitnetlinear_kernel(tc, x, weight, bias, out):
                         k = s_col["n"]
                         s_col["n"] = k + 1
                         nc.scalar.activation(
-                            out=s_abs[:, lo:hi], in_=src[:, lo:hi], func=ACT.Abs, accum_out=part_s[:, k : k + 1]
+                            out=g_t[N_U - 1 - k % 6][:, 0 : hi - lo], in_=src[:, lo:hi], func=ACT.Abs, accum_out=part_s[:, k : k + 1]
                         )
                         continue
                     if i not in abs_t:

@@ -245,7 +245,10 @@ def tile_bitnetlinear_kernel(tc, x, weight, bias, out):
                 nc.scalar.copy(out=xv[:, 2 * b : 2 * b + 2, :, :], in_=bank_view(tb))
             xg_tiles[m] = xg
             if m == N_XT - 1:
-                nc.sync.dma_start(out=bias_bc[:], in_=bias.partition_broadcast(P))
+                for lo in range(0, D_OUT, 2 * P):
+                    nc.sync.dma_start(
+                        out=bias_bc[:, lo : lo + 2 * P], in_=bias[lo : lo + 2 * P].partition_broadcast(P)
+                    )
 
         def x_quant(m):
             sl = slice(512 * m, 512 * (m + 1))

from contextlib import ExitStack

import concourse.mybir as mybir
from concourse.masks import make_identity

F32 = mybir.dt.float32
BF16 = mybir.dt.bfloat16
I32 = mybir.dt.int32
U32 = mybir.dt.uint32
U8 = mybir.dt.uint8
FP8X4 = mybir.dt.float8_e4m3fn_x4
ALU = mybir.AluOpType
ACT = mybir.ActivationFunctionType
AX = mybir.AxisListType

P = 128
M_ROWS = 1024
D_IN = 2048
D_OUT = 2048
N_W = D_OUT * D_IN
FLOPS = 2 * M_ROWS * D_IN * D_OUT

N_OT = 16
N_XT = 8
GROUPS = ((0, 1), (2, 3), (4, 5), (6, 7), (8, 9), (10, 11), (12, 13), (14,), (15,))
S_HALVES = tuple((i, h) for i in (0, 2, 4, 6, 8, 10, 12) for h in range(2)) + ((14, 0),)
N_PROMPT = 8
N_EARLY = 10
S_COPY = ((8, 0), (8, 1), (9, 0), (9, 1))
COPY_LAG = 1
SUM_LAG = 1
V_P1_UNITS = (0, 1, 2, 3, 4)
S_P3_UNITS = (13, 14, 15)
LATE_WITH = {2: (10,), 3: (11, 12), 4: (13, 14), 5: (15,)}
XQ_FIRST = 0
X_BEFORE = 4
S_P1_AT = {}
FILL_FROM = 2
R6_KEEP = 3
HALVED = (15,)
N_NAT = 7
ACC_BANKS = (4, 5, 6, 7, 2, 3)
LATE_BANKS = (0, 1)
X_BANKS = (0, 1, 2, 3)
W_BANKS = (0, 1, 2, 3, 4, 5)
EDGE = (2.0 - 2.0**-8) * (1.0 - 2.0**-21)
SIGN_AND_TWO = -0x3FFF4000


def tile_bitnetlinear_kernel(tc, x, weight, bias, out):
    nc = tc.nc
    xf = x.flatten_outer_dims()
    of = out.flatten_outer_dims()
    with ExitStack() as ctx:
        ctx.enter_context(tc.manual_schedule())
        const = ctx.enter_context(tc.tile_pool(name="const", bufs=1))
        keep = ctx.enter_context(tc.tile_pool(name="keep", bufs=1))
        gpool = ctx.enter_context(tc.tile_pool(name="gpool", bufs=16))
        apool = ctx.enter_context(tc.tile_pool(name="apool", bufs=8))
        obp = ctx.enter_context(tc.tile_pool(name="obp", bufs=8))
        nat = ctx.enter_context(tc.tile_pool(name="nat", bufs=N_NAT))
        psum = ctx.enter_context(tc.psum_pool(name="psum", bufs=1))

        load_list = [("w", q) for q in range(N_OT // 2)] + [("x", q) for q in range(N_XT // 2)]
        nat_tiles = {}
        st = {"load": 0, "bank": 0}

        def load_next():
            k = st["load"]
            if k >= len(load_list):
                return
            st["load"] = k + 1
            kind, q = load_list[k]
            t = nat.tile([P, 2 * D_IN], BF16, tag="nat", name="nat_%s%d" % (kind, q))
            src = weight if kind == "w" else xf
            rows = src[2 * P * q : 2 * P * (q + 1), :]
            for j in range(2):
                nat_tiles[(kind, 2 * q + j)] = t[:, D_IN * j : D_IN * (j + 1)]
            if kind == "w" and q == N_OT // 2 - 1:
                nc.sync.dma_start(out=t[:, 0:D_IN], in_=rows[0:P, :])
                for h in range(2):
                    lo = D_IN // 2 * h
                    nc.sync.dma_start(out=t[:, D_IN + lo : D_IN + lo + D_IN // 2], in_=rows[P : 2 * P, lo : lo + D_IN // 2])
            elif q == 0:
                by_row = rows.rearrange("(p j) i -> p j i", j=2)
                for j in range(2):
                    nc.sync.dma_start(out=t[:, D_IN * j : D_IN * (j + 1)], in_=by_row[:, j, :])
            else:
                nc.sync.dma_start(out=t[:], in_=rows.rearrange("(p j) i -> p (j i)", j=2))

        for k in range(N_NAT):
            load_next()

        ident = const.tile([P, P], F32, name="ident")
        make_identity(nc, ident[:])
        ones_bf = const.tile([P, P], BF16, name="ones_bf")
        nc.vector.memset(ones_bf[:], 1.0 / N_W)
        ones_f = const.tile([P, P], F32, name="ones_f")
        nc.vector.memset(ones_f[:], 1.0 / N_W)
        junk = const.tile([P, 1], F32, name="junk")
        nc.vector.memset(junk[:], 0.0)
        junk2 = const.tile([P, 1], F32, name="junk2")
        nc.scalar.activation(out=junk2[:], in_=junk[:], func=ACT.Abs)
        part_s = const.tile([P, 16], F32, name="part_s")
        nc.vector.memset(part_s[:], 0.0)
        bias_bc = const.tile([P, D_OUT], BF16, name="bias_bc")

        w_codes = keep.tile([P, 4 * D_OUT], U32, name="w_codes", align_bytes=64)
        w_scales = keep.tile([P, 4 * D_OUT], U8, name="w_scales", align_bytes=64)
        x_codes = keep.tile([P, 4 * M_ROWS], U32, name="x_codes", align_bytes=64)
        x_scales = keep.tile([P, 4 * M_ROWS], U8, name="x_scales", align_bytes=64)
        g_t = [gpool.tile([P, 2048], BF16, tag="g", name="g%d" % i, align_bytes=64) for i in range(N_OT)]

        sum_ps = psum.tile([P, 512], F32, tag="b6", name="sum_ps")

        group_of = {}
        first_unit = []
        unit_group = []
        for g, tiles in enumerate(GROUPS):
            first_unit.append(len(unit_group))
            for pos, i in enumerate(tiles):
                group_of[i] = (g, pos)
                unit_group.append(g)
        N_U = len(unit_group)

        def unit_tiles(u):
            return GROUPS[unit_group[u]]

        def half_transposes(kind, idx, b, bank):
            sv = nat_tiles[(kind, idx)].bitcast(F32)
            st["bank"] = st["bank"] + 1
            tb = psum.tile([P, 512], F32, tag="b%d" % bank, name="tp%d" % st["bank"])
            for q in range(4):
                lo = 512 * b + 128 * q
                nc.tensor.transpose(tb[:, 128 * q : 128 * (q + 1)], sv[:, lo : lo + 128], ident[:])
            return tb

        def bank_view(tb):
            return tb[:].rearrange("p (c u o) -> p c o u", c=2, u=2)

        def w_unit_part(i, b):
            g, pos = group_of[i]
            if len(GROUPS[g]) == 2:
                return first_unit[g] + b, 0, 2, 128 * pos, 256
            return first_unit[g], 2 * b, 4, 0, 128

        def w_dst(i, b):
            u, c0, cs, o0, ow = w_unit_part(i, b)
            v = g_t[u][:].bitcast(F32).rearrange("p (c o u) -> p c o u", c=cs, u=2)
            return v[:, c0 : c0 + 2, o0 : o0 + 128, :]

        w_bank = {}
        wb = {"n": 0}

        def w_transposes(i):
            for b in range(2):
                w_bank[(i, b)] = half_transposes("w", i, b, W_BANKS[wb["n"] % len(W_BANKS)])
                wb["n"] = wb["n"] + 1

        def w_copy(i):
            for b in range(2):
                if (i, b) in S_COPY:
                    nc.scalar.copy(out=w_dst(i, b), in_=bank_view(w_bank[(i, b)]))
                else:
                    nc.vector.tensor_copy(out=w_dst(i, b), in_=bank_view(w_bank[(i, b)]))

        abs_t = {}
        s_col = {"n": 0}
        v_halves = [(i, h) for i in range(N_OT) for h in range(2) if (i, h) not in S_HALVES]
        HALF = D_IN // 2

        def abs_tile(i):
            src = nat_tiles[("w", i)]
            for mine in (True, False):
                hs = [h for h in range(2) if ((i, h) in S_HALVES) == mine]
                spans = [(HALF * h, HALF * (h + 1)) for h in hs]
                if len(hs) == 2 and i not in HALVED:
                    spans = [(0, D_IN)]
                for lo, hi in spans:
                    if mine:
                        k = s_col["n"]
                        s_col["n"] = k + 1
                        nc.scalar.activation(
                            out=g_t[N_U - 1 - k % 6][:, 0 : hi - lo], in_=src[:, lo:hi], func=ACT.Abs, accum_out=part_s[:, k : k + 1]
                        )
                        continue
                    if i not in abs_t:
                        abs_t[i] = apool.tile([P, 2048], BF16, tag="a", name="a%d" % i, align_bytes=64)
                    nc.vector.tensor_scalar(
                        out=abs_t[i][:, lo:hi].bitcast(I32), in0=src[:, lo:hi].bitcast(I32),
                        scalar1=0x7FFF7FFF, scalar2=None, op0=ALU.bitwise_and,
                    )

        def sum_tile(i):
            for h in range(2):
                if (i, h) in S_HALVES:
                    continue
                for c in range(4):
                    lo = HALF * h + 256 * c
                    nc.tensor.matmul(
                        sum_ps[:, 0:256], lhsT=ones_bf[:], rhs=abs_t[i][:, lo : lo + 256],
                        start=((i, h) == v_halves[0] and c == 0), stop=((i, h) == v_halves[-1] and c == 3),
                    )

        for i in range(N_OT):
            abs_tile(i)
            if 0 <= i - COPY_LAG < N_PROMPT:
                w_copy(i - COPY_LAG)
            if i < N_EARLY:
                w_transposes(i)
            if i >= SUM_LAG:
                sum_tile(i - SUM_LAG)
            if i % 2 == 1:
                load_next()
        for i in range(N_OT - SUM_LAG, N_OT):
            sum_tile(i)
        nc.tensor.matmul(sum_ps[:, 256:272], lhsT=ones_f[:], rhs=part_s[:], start=True, stop=True)
        for i in range(N_PROMPT, N_EARLY):
            w_copy(i)

        mean = const.tile([P, 1], F32, name="mean")
        nc.vector.tensor_reduce(out=mean[:], in_=sum_ps[:, 0:272], axis=AX.X, op=ALU.add)
        scale = const.tile([P, 1], F32, name="scale")
        nc.vector.tensor_scalar(
            out=scale[:], in0=mean[:], scalar1=1e-5, scalar2=1000.0, op0=ALU.max, op1=ALU.min
        )
        inv = const.tile([P, 1], F32, name="inv")
        nc.vector.reciprocal(out=inv[:], in_=scale[:])
        up = const.tile([P, 1], F32, name="up")
        half = const.tile([P, 1], F32, name="half")

        def late_scalars():
            nc.vector.tensor_scalar(out=up[:], in0=inv[:], scalar1=1.5 * EDGE, scalar2=None, op0=ALU.mult)
            nc.vector.tensor_scalar(out=half[:], in0=scale[:], scalar1=0.5, scalar2=None, op0=ALU.mult)

        xg_tiles = {}
        xb = {"n": 0}

        def x_tile(m):
            xg = apool.tile([P, 2048], BF16, tag="a", name="xg%d" % m, align_bytes=64)
            xv = xg[:].bitcast(F32).rearrange("p (c o u) -> p c o u", c=4, u=2)
            for b in range(2):
                tb = half_transposes("x", m, b, X_BANKS[xb["n"] % len(X_BANKS)])
                xb["n"] = xb["n"] + 1
                nc.scalar.copy(out=xv[:, 2 * b : 2 * b + 2, :, :], in_=bank_view(tb))
            xg_tiles[m] = xg
            if m == N_XT - 1:
                for lo in range(0, D_OUT, 2 * P):
                    nc.sync.dma_start(
                        out=bias_bc[:, lo : lo + 2 * P], in_=bias[lo : lo + 2 * P].partition_broadcast(P)
                    )

        def x_quant(m):
            sl = slice(512 * m, 512 * (m + 1))
            nc.vector.quantize_mx(out=x_codes[:, sl].bitcast(FP8X4), scales=x_scales[:, sl], in_=xg_tiles[m][:])

        def late_unit(u):
            tiles = unit_tiles(u)
            for k in range(2):
                i, b = (tiles[k], u - first_unit[unit_group[u]]) if len(tiles) == 2 else (tiles[0], k)
                tb = half_transposes("w", i, b, LATE_BANKS[k])
                uu, c0, cs, o0, ow = w_unit_part(i, b)
                for c in range(2):
                    lo = 4 * ((c0 + c) * ow + o0)
                    nc.scalar.activation(
                        out=g_t[u][:, lo : lo + 512].rearrange("p (o u e) -> p o u e", u=2, e=2),
                        in_=tb[:, 256 * c : 256 * (c + 1)].bitcast(BF16).rearrange("p (u o e) -> p o u e", u=2, e=2),
                        func=ACT.Copy, scale=up[:, 0:1],
                    )

        def p1(u):
            if u in V_P1_UNITS:
                nc.vector.tensor_scalar(
                    out=g_t[u][:], in0=g_t[u][:], scalar1=inv[:, 0:1], scalar2=1.5 * EDGE, op0=ALU.mult, op1=ALU.mult
                )

        def p2(u):
            nc.vector.tensor_scalar(
                out=g_t[u][:].bitcast(I32), in0=g_t[u][:].bitcast(I32),
                scalar1=SIGN_AND_TWO, scalar2=None, op0=ALU.bitwise_and,
            )

        def p3(u):
            if u in S_P3_UNITS:
                nc.scalar.activation(out=g_t[u][:], in_=g_t[u][:], func=ACT.Copy, scale=half[:, 0:1])
            else:
                nc.vector.tensor_scalar(out=g_t[u][:], in0=g_t[u][:], scalar1=half[:, 0:1], scalar2=None, op0=ALU.mult)

        def q_op(u):
            sl = slice(512 * u, 512 * (u + 1))
            nc.vector.quantize_mx(out=w_codes[:, sl].bitcast(FP8X4), scales=w_scales[:, sl], in_=g_t[u][:])

        opened = []
        stored = set()
        closed = []
        acc = {}
        ph = {"xt": 0, "xq": 0, "pb": 0, "r6": 0}

        def mx_group(g, m):
            width = 128 * len(GROUPS[g])
            per_bank = 2
            key = (g, m // per_bank)
            if key not in acc:
                if ph["pb"] >= len(ACC_BANKS):
                    old = opened[ph["pb"] - len(ACC_BANKS)]
                    while old not in stored:
                        r6_next()
                bank = ACC_BANKS[ph["pb"] % len(ACC_BANKS)]
                ph["pb"] = ph["pb"] + 1
                opened.append(key)
                acc[key] = psum.tile([P, 512], F32, tag="b%d" % bank, name="acc%d_%d" % key)
            col = width * (m % per_bank)
            for c in range(4):
                xs = slice(512 * m + 128 * c, 512 * m + 128 * (c + 1))
                lo = 512 * first_unit[g] + width * c
                ws = slice(lo, lo + width)
                nc.tensor.matmul_mx(
                    out=acc[key][:, col : col + width],
                    lhsT=x_codes[:, xs].bitcast(FP8X4), lhsT_scale=x_scales[:, xs],
                    rhs=w_codes[:, ws].bitcast(FP8X4), rhs_scale=w_scales[:, ws],
                    start=(c == 0), stop=(c == 3),
                )

        def r6(g, h):
            width = 128 * len(GROUPS[g])
            o0 = P * GROUPS[g][0]
            ob = obp.tile([P, 512], F32, tag="ob", name="ob%d_%d" % (g, h), align_bytes=64)
            flat = ob[:, 0 : 2 * width]
            b_row = bias_bc[:, o0 : o0 + width]
            ps = acc[(g, h)][:, 0 : 2 * width]
            if len(GROUPS[g]) == 2:
                nc.vector.tensor_tensor(
                    out=flat.rearrange("p (t q j) -> p t q j", t=2, j=2),
                    in0=ps.rearrange("p (t j q) -> p t q j", t=2, j=2),
                    in1=b_row.rearrange("p (q j) -> p q j", j=2).unsqueeze(1).to_broadcast([P, 2, P, 2]),
                    op=ALU.add,
                )
            else:
                nc.vector.tensor_tensor(
                    out=flat.rearrange("p (t o) -> p t o", t=2),
                    in0=ps.rearrange("p (t o) -> p t o", t=2),
                    in1=b_row.unsqueeze(1).to_broadcast([P, 2, width]),
                    op=ALU.add,
                )
            nc.sync.dma_start(
                out=of[256 * h : 256 * (h + 1), o0 : o0 + width].rearrange("(p t) o -> p t o", t=2),
                in_=flat.rearrange("p (t o) -> p t o", t=2),
            )

        def r6_next():
            g, h = closed[ph["r6"]]
            ph["r6"] = ph["r6"] + 1
            stored.add((g, h))
            r6(g, h)

        def s_p1(u):
            if u not in V_P1_UNITS and unit_tiles(u)[-1] < N_EARLY:
                nc.scalar.activation(out=g_t[u][:], in_=g_t[u][:], func=ACT.Copy, scale=up[:, 0:1])

        def p2_s(u):
            p2(u)
            p3(u)

        def units(g):
            if not 0 <= g < len(GROUPS):
                return []
            return [first_unit[g] + k for k in range(len(GROUPS[g]))]

        def mx_tokens(g, m):
            per_bank = 2
            mx_group(g, m)
            if m % per_bank == per_bank - 1:
                closed.append((g, m // per_bank))

        for m in range(X_BEFORE):
            x_tile(m)
        for u in units(0):
            p1(u)
        late_scalars()
        for m in range(X_BEFORE, N_XT):
            if m in S_P1_AT:
                s_p1(S_P1_AT[m])
            x_tile(m)
        for u in range(N_U):
            if u not in S_P1_AT.values():
                s_p1(u)
        for u in units(0):
            p2(u)
        for m in range(XQ_FIRST):
            x_quant(m)
        for u in units(0):
            p3(u)
        for u in units(0):
            q_op(u)
        fill = [(p1, u) for u in units(1)] + [(p2, u) for u in units(1)]
        for m in range(N_XT):
            if m >= XQ_FIRST:
                x_quant(m)
                if fill and m >= FILL_FROM:
                    f, u = fill.pop(0)
                    f(u)
            mx_tokens(0, m)
        for f, u in fill:
            f(u)
        for g in range(1, len(GROUPS)):
            before = [(p3, u) for u in units(g) if u not in S_P3_UNITS] + [(q_op, u) for u in units(g)]
            after = [(p1, u) for u in units(g + 1) if u in V_P1_UNITS]
            after = after + [(p2, u) for u in units(g + 1) if u not in S_P3_UNITS]
            after = after + [(p2_s, u) for u in units(g + 2) if u in S_P3_UNITS]
            n_r6 = max(0, len(closed) - ph["r6"] - R6_KEEP)
            n_before = n_r6 // 2 if g > 1 else 0
            k = 0
            for f, u in before:
                f(u)
                if k >= 1 and n_before > 0:
                    r6_next()
                    n_before = n_before - 1
                    n_r6 = n_r6 - 1
                k = k + 1
            late = LATE_WITH.get(g, ())
            for m in range(N_XT):
                if m % 4 == 0 and m // 4 < len(late):
                    late_unit(late[m // 4])
                mx_tokens(g, m)
            for f, u in after:
                f(u)
                if n_r6 > 0:
                    r6_next()
                    n_r6 = n_r6 - 1
            while n_r6 > 0:
                r6_next()
                n_r6 = n_r6 - 1
        while ph["r6"] < len(closed):
            r6_next()
